import numpy as np
import ml_dtypes


def mxq(x, axis, fmt="e4m3"):
    dtype, down = {"e4m3": (ml_dtypes.float8_e4m3fn, 7), "e5m2": (ml_dtypes.float8_e5m2, 14)}[fmt]
    v = np.moveaxis(np.asarray(x, np.float32).astype(ml_dtypes.bfloat16).astype(np.float64), axis, -1)
    blocks = v.reshape(v.shape[:-1] + (-1, 32))
    amax = np.abs(blocks).max(-1, keepdims=True)
    byte = np.maximum(np.where(amax > 0, np.frexp(amax)[1] - 1 + 127, 0) - down, 1)
    scale = np.exp2(byte - 127.0)
    codes = (blocks / scale).astype(np.float32).astype(dtype).astype(np.float64)
    return np.moveaxis((codes * scale).reshape(v.shape), -1, axis)


WIDE = False


def mx_kscale(k):
    if not WIDE:
        return np.ones(k)
    levels = np.array([10, -10, 5, -5, 0])
    a = np.random.permutation(np.resize(levels, k // 512 * 4)).reshape(k // 512, 4)
    idx = np.arange(k)
    return np.exp2(a[idx // 512, idx % 128 // 32])


BF16 = ml_dtypes.bfloat16


def bf(x):
    return np.asarray(x, np.float32).astype(BF16)


def f64(x):
    return np.asarray(x).astype(np.float64)


B, C_IN, C_OUT, HEADS, H, W = 2, 1024, 1024, 8, 16, 32
DH = C_OUT // HEADS
M = H * W


def setup_inputs():
    s = mx_kscale(C_IN)
    return {
        "vh": bf(np.random.standard_normal((B, HEADS, DH, M)) * 2.0),
        "zh": bf(np.random.standard_normal((B, HEADS, DH, M))),
        "r_pos": bf(np.random.standard_normal((HEADS, DH, M)) * np.sqrt(0.5)),
        "x": bf(np.random.standard_normal((B, C_IN, H, W)) * s[None, :, None, None]),
        "w_q": bf(np.random.standard_normal((C_OUT, C_IN)) * 2.0 / np.sqrt(C_IN) / s[None, :]),
    }


def reference(vh, zh, r_pos, x, w_q):
    vt = f64(vh).transpose(0, 1, 3, 2)
    scores = vt @ f64(zh) + vt @ f64(r_pos)
    sc = scores / np.sqrt(DH)
    e = np.exp(sc - sc.max(-1, keepdims=True))
    xf = f64(x).reshape(B, C_IN, M)
    qh = (mxq(f64(w_q), 1, "e4m3") @ mxq(xf, 1, "e4m3")).reshape(B, HEADS, DH, M)
    o = (mxq(e, 3, "e4m3") @ mxq(qh, 3, "e4m3").transpose(0, 1, 3, 2)) / e.sum(-1, keepdims=True)
    return o.transpose(0, 1, 3, 2).reshape(B, C_OUT, H, W)

@@ -1,0 +1,285 @@
+from contextlib import ExitStack
+
+import concourse.mybir as mybir
+from concourse.masks import make_identity
+
+BF16 = mybir.dt.bfloat16
+F32 = mybir.dt.float32
+U32 = mybir.dt.uint32
+U8 = mybir.dt.uint8
+FP8X4 = mybir.dt.float8_e4m3fn_x4
+ACT = mybir.ActivationFunctionType
+ALU = mybir.AluOpType
+AXIS = mybir.AxisListType
+
+P = 128
+PACK = 4
+BATCH, HEADS, DH, PIX = 2, 8, 128, 512
+C_IN = 1024
+K_PASSES = C_IN // (P * PACK)
+UNITS = BATCH * HEADS
+ROW_TILES = PIX // P
+SCALE = 1.0 / DH**0.5
+
+FLOPS = 2 * UNITS * PIX * PIX * DH * 3 + 2 * BATCH * HEADS * DH * C_IN * PIX
+
+
+def tile_multiheadselfattention2d_pa_kernel(tc, vh, zh, r_pos, x, w_q, out):
+    nc = tc.nc
+    with ExitStack() as ctx:
+        consts = ctx.enter_context(tc.tile_pool(name="consts", bufs=1))
+        inputs = ctx.enter_context(tc.tile_pool(name="inputs", bufs=1))
+        kept = ctx.enter_context(tc.tile_pool(name="kept", bufs=1))
+        stage = ctx.enter_context(tc.tile_pool(name="stage", bufs=2))
+        ring = ctx.enter_context(tc.tile_pool(name="ring", bufs=4))
+        psum_s = ctx.enter_context(tc.psum_pool(name="psum_s", bufs=3))
+        psum_e = ctx.enter_context(tc.psum_pool(name="psum_e", bufs=2))
+        psum_m = ctx.enter_context(tc.psum_pool(name="psum_m", bufs=3))
+
+        vh_sb, zh_sb, r_sb, w_sb, x_sb = {}, {}, {}, {}, {}
+
+        def load_unit(i):
+            b, hd = divmod(i, HEADS)
+            vh_sb[i] = inputs.tile([P, PIX], BF16, name="vh_sb%d" % i)
+            nc.sync.dma_start(out=vh_sb[i][:], in_=vh[b, hd])
+            zh_sb[i] = inputs.tile([P, PIX], BF16, name="zh_sb%d" % i)
+            nc.sync.dma_start(out=zh_sb[i][:], in_=zh[b, hd])
+            if b == 0:
+                r_sb[hd] = inputs.tile([P, PIX], BF16, name="r_sb%d" % hd)
+                nc.sync.dma_start(out=r_sb[hd][:], in_=r_pos[hd])
+
+        def load_x(b):
+            x_sb[b] = inputs.tile([P, K_PASSES, PACK, PIX], BF16, name="x_sb%d" % b)
+            nc.sync.dma_start(
+                out=x_sb[b][:].rearrange("q g (u e) n -> q (g u) (e n)", e=2),
+                in_=x[b].rearrange("(g u q e) h w -> q (g u) (e h w)", g=K_PASSES, u=2, e=2),
+            )
+
+        def load_w(hd):
+            w_sb[hd] = inputs.tile([P, C_IN], BF16, name="w_sb%d" % hd)
+            nc.sync.dma_start(out=w_sb[hd][:], in_=w_q[hd * DH : (hd + 1) * DH, :])
+
+        load_unit(0)
+        load_unit(1)
+        load_x(0)
+        load_w(0)
+        load_w(1)
+        for hd in range(2, HEADS):
+            load_unit(hd)
+            load_w(hd)
+        load_x(1)
+        for i in range(HEADS, UNITS):
+            load_unit(i)
+
+        ident_bf = consts.tile([P, P], BF16)
+        make_identity(nc, ident_bf[:])
+        ident_f32 = consts.tile([P, P], F32)
+        make_identity(nc, ident_f32[:])
+        warm = consts.tile([P, 1], F32)
+        nc.vector.memset(warm[:], 0.0)
+        warm_out = consts.tile([P, 1], F32)
+        nc.scalar.activation(out=warm_out[:], in_=warm[:], func=ACT.Exp)
+
+        x_codes = kept.tile([P, BATCH, K_PASSES, PIX], U32, align_bytes=64)
+        x_scales = kept.tile([P, BATCH, K_PASSES, PIX], U8, align_bytes=64)
+        x_grouped = {}
+
+        def regroup_x(b, g):
+            grouped = stage.tile([P, PIX, PACK], BF16, name="x_grouped", align_bytes=64)
+            nc.vector.tensor_copy(
+                out=grouped[:].rearrange("q (c i) t -> q c t i", i=4),
+                in_=x_sb[b][:, g].rearrange("q t (c i) -> q c t i", i=4),
+            )
+            x_grouped[b, g] = grouped
+
+        def quantise_x(b, g):
+            nc.vector.quantize_mx(
+                out=x_codes[:, b, g, :].bitcast(FP8X4),
+                scales=x_scales[:, b, g, :],
+                in_=x_grouped[b, g][:].rearrange("q n t -> q (n t)"),
+            )
+
+        w_codes = kept.tile([P, HEADS, K_PASSES, DH], U32, align_bytes=64)
+        w_scales = kept.tile([P, HEADS, K_PASSES, DH], U8, align_bytes=64)
+        w_grouped = {}
+
+        def transpose_w(hd):
+            w_words = w_sb[hd][:].bitcast(F32)
+            wT_ps = psum_m.tile([P, K_PASSES, 2, DH], F32, name="wT_ps", tag="misc")
+            for g in range(K_PASSES):
+                for u in range(2):
+                    first = (2 * g + u) * P
+                    nc.tensor.transpose(
+                        out=wT_ps[:, g, u, :], in_=w_words[:, first : first + P], identity=ident_f32[:]
+                    )
+            grouped = stage.tile([P, K_PASSES, DH, PACK], BF16, name="w_grouped", align_bytes=64)
+            nc.vector.tensor_copy(
+                out=grouped[:].bitcast(F32), in_=wT_ps[:].rearrange("q g u c -> q g c u")
+            )
+            w_grouped[hd] = grouped
+
+        def quantise_w(hd):
+            nc.vector.quantize_mx(
+                out=w_codes[:, hd].rearrange("q g c -> q (g c)").bitcast(FP8X4),
+                scales=w_scales[:, hd].rearrange("q g c -> q (g c)"),
+                in_=w_grouped[hd][:].rearrange("q g c t -> q (g c t)"),
+            )
+
+        q_grouped, q_codes, q_scales = {}, {}, {}
+
+        def project_values(i):
+            b, hd = divmod(i, HEADS)
+            qT_ps = psum_m.tile([P, PACK, DH], F32, name="qT_ps", tag="misc")
+            for t in range(PACK):
+                pixels = slice(t * P, (t + 1) * P)
+                for g in range(K_PASSES):
+                    nc.tensor.matmul_mx(
+                        out=qT_ps[:, t, :],
+                        lhsT=x_codes[:, b, g, pixels].bitcast(FP8X4),
+                        lhsT_scale=x_scales[:, b, g, pixels],
+                        rhs=w_codes[:, hd, g, :].bitcast(FP8X4),
+                        rhs_scale=w_scales[:, hd, g, :],
+                        start=(g == 0),
+                        stop=(g == K_PASSES - 1),
+                    )
+            grouped = stage.tile([P, DH, PACK], BF16, name="q_grouped", align_bytes=64)
+            nc.scalar.copy(out=grouped[:], in_=qT_ps[:].rearrange("p t d -> p d t"))
+            q_grouped[i] = grouped
+
+        def quantise_q(i):
+            q_codes[i] = ring.tile([P, DH], U32, name="q_codes", align_bytes=64)
+            q_scales[i] = ring.tile([P, DH], U8, name="q_scales", align_bytes=64)
+            nc.vector.quantize_mx(
+                out=q_codes[i][:].bitcast(FP8X4),
+                scales=q_scales[i][:],
+                in_=q_grouped[i][:].rearrange("p d t -> p (d t)"),
+            )
+
+        e_rows, row_sum = {}, {}
+
+        def scores_and_exp(i, mt):
+            hd = i % HEADS
+            queries = slice(mt * P, (mt + 1) * P)
+            s_ps = psum_s.tile([P, PIX], F32, name="s_ps")
+            nc.tensor.matmul(out=s_ps[:], lhsT=vh_sb[i][:, queries], rhs=zh_sb[i][:], start=True, stop=False)
+            nc.tensor.matmul(out=s_ps[:], lhsT=vh_sb[i][:, queries], rhs=r_sb[hd][:], start=False, stop=True)
+            row_max = ring.tile([P, 1], F32, name="row_max")
+            nc.vector.reduce_max(out=row_max[:], in_=s_ps[:], axis=AXIS.X)
+            shift = ring.tile([P, 1], F32, name="shift")
+            nc.gpsimd.tensor_scalar(
+                out=shift[:], in0=row_max[:], scalar1=-SCALE, scalar2=0.0, op0=ALU.mult, op1=ALU.add
+            )
+            if mt == 0:
+                row_sum[i] = ring.tile([P, ROW_TILES], F32, name="row_sum")
+            if mt % 2 == 0:
+                e_rows[i, mt // 2] = ring.tile([P, 2, PIX], BF16, name="e_rows")
+            nc.scalar.activation(
+                out=e_rows[i, mt // 2][:, mt % 2, :],
+                in_=s_ps[:],
+                func=ACT.Exp,
+                bias=shift[:],
+                scale=SCALE,
+                accum_out=row_sum[i][:, mt : mt + 1],
+            )
+
+        e_grouped, e_codes, e_scales = {}, {}, {}
+
+        def transpose_e(i, half):
+            eT_ps = psum_e.tile([P, 2, PACK, P], BF16, name="eT_ps")
+            for a in range(2):
+                for t in range(PACK):
+                    nc.tensor.transpose(
+                        out=eT_ps[:, a, t, :],
+                        in_=e_rows[i, half][:, a, t * P : (t + 1) * P],
+                        identity=ident_bf[:],
+                    )
+            if half == 0:
+                e_grouped[i] = stage.tile([P, ROW_TILES, P, PACK], BF16, name="e_grouped", align_bytes=64)
+            nc.scalar.copy(
+                out=e_grouped[i][:, 2 * half : 2 * half + 2],
+                in_=eT_ps[:].rearrange("p a t m -> p a m t"),
+            )
+
+        def quantise_e(i):
+            e_codes[i] = ring.tile([P, PIX], U32, name="e_codes", align_bytes=64)
+            e_scales[i] = ring.tile([P, PIX], U8, name="e_scales", align_bytes=64)
+            nc.vector.quantize_mx(
+                out=e_codes[i][:].bitcast(FP8X4),
+                scales=e_scales[i][:],
+                in_=e_grouped[i][:].rearrange("p a m t -> p (a m t)"),
+            )
+
+        o_sb = {}
+
+        def attend(i):
+            inv_sum = ring.tile([P, ROW_TILES], F32, name="inv_sum")
+            nc.vector.reciprocal(out=inv_sum[:], in_=row_sum[i][:])
+            o_ps = psum_m.tile([P, ROW_TILES, DH], F32, name="o_ps", tag="misc")
+            for mt in range(ROW_TILES):
+                queries = slice(mt * P, (mt + 1) * P)
+                nc.tensor.matmul_mx(
+                    out=o_ps[:, mt, :],
+                    lhsT=e_codes[i][:, queries].bitcast(FP8X4),
+                    lhsT_scale=e_scales[i][:, queries],
+                    rhs=q_codes[i][:].bitcast(FP8X4),
+                    rhs_scale=q_scales[i][:],
+                    start=True,
+                    stop=True,
+                )
+            o_sb[i] = stage.tile([P, ROW_TILES, DH], F32, name="o_sb")
+            nc.vector.tensor_tensor(
+                out=o_sb[i][:],
+                in0=o_ps[:],
+                in1=inv_sum[:].unsqueeze(2).to_broadcast([P, ROW_TILES, DH]),
+                op=ALU.mult,
+            )
+
+        def store_unit(i):
+            b, hd = divmod(i, HEADS)
+            oT_ps = psum_m.tile([P, PIX], F32, name="oT_ps", tag="misc")
+            for mt in range(ROW_TILES):
+                nc.tensor.transpose(
+                    out=oT_ps[:, mt * P : (mt + 1) * P], in_=o_sb[i][:, mt, :], identity=ident_f32[:]
+                )
+            out_sb = ring.tile([P, PIX], F32, name="out_sb")
+            nc.vector.tensor_copy(out=out_sb[:], in_=oT_ps[:])
+            nc.sync.dma_start(
+                out=out[b, hd * DH : (hd + 1) * DH].rearrange("c h w -> c (h w)"), in_=out_sb[:]
+            )
+
+        for i in range(UNITS + 2):
+            scoring = i < UNITS
+            if scoring:
+                scores_and_exp(i, 0)
+            if 1 <= i <= UNITS:
+                project_values(i - 1)
+            if i >= 2:
+                attend(i - 2)
+            if i in (0, HEADS - 1):
+                regroup_x(i // (HEADS - 1), 0)
+
+            if scoring:
+                scores_and_exp(i, 1)
+            if 1 <= i <= UNITS:
+                transpose_e(i - 1, 1)
+                quantise_q(i - 1)
+            if i in (0, HEADS - 1):
+                regroup_x(i // (HEADS - 1), 1)
+                quantise_x(i // (HEADS - 1), 0)
+
+            if scoring:
+                scores_and_exp(i, 2)
+            if i < HEADS:
+                transpose_w(i)
+            if i >= 2:
+                store_unit(i - 2)
+            if 1 <= i <= UNITS:
+                quantise_e(i - 1)
+            if i in (0, HEADS - 1):
+                quantise_x(i // (HEADS - 1), 1)
+
+            if scoring:
+                scores_and_exp(i, 3)
+                transpose_e(i, 0)
+            if i < HEADS:
+                quantise_w(i)

@@ -30,7 +30,7 @@ def tile_multiheadselfattention2d_pa_kernel(tc, vh, zh, r_pos, x, w_q, out):
         consts = ctx.enter_context(tc.tile_pool(name="consts", bufs=1))
         inputs = ctx.enter_context(tc.tile_pool(name="inputs", bufs=1))
         kept = ctx.enter_context(tc.tile_pool(name="kept", bufs=1))
-        stage = ctx.enter_context(tc.tile_pool(name="stage", bufs=2))
+        stage = ctx.enter_context(tc.tile_pool(name="stage", bufs=3))
         ring = ctx.enter_context(tc.tile_pool(name="ring", bufs=4))
         psum_s = ctx.enter_context(tc.psum_pool(name="psum_s", bufs=3))
         psum_e = ctx.enter_context(tc.psum_pool(name="psum_e", bufs=2))
@@ -113,9 +113,7 @@ def tile_multiheadselfattention2d_pa_kernel(tc, vh, zh, r_pos, x, w_q, out):
                         out=wT_ps[:, g, u, :], in_=w_words[:, first : first + P], identity=ident_f32[:]
                     )
             grouped = stage.tile([P, K_PASSES, DH, PACK], BF16, name="w_grouped", align_bytes=64)
-            nc.vector.tensor_copy(
-                out=grouped[:].bitcast(F32), in_=wT_ps[:].rearrange("q g u c -> q g c u")
-            )
+            nc.scalar.copy(out=grouped[:].bitcast(F32), in_=wT_ps[:].rearrange("q g u c -> q g c u"))
             w_grouped[hd] = grouped
 
         def quantise_w(hd):
@@ -166,9 +164,7 @@ def tile_multiheadselfattention2d_pa_kernel(tc, vh, zh, r_pos, x, w_q, out):
             row_max = ring.tile([P, 1], F32, name="row_max")
             nc.vector.reduce_max(out=row_max[:], in_=s_ps[:], axis=AXIS.X)
             shift = ring.tile([P, 1], F32, name="shift")
-            nc.gpsimd.tensor_scalar(
-                out=shift[:], in0=row_max[:], scalar1=-SCALE, scalar2=0.0, op0=ALU.mult, op1=ALU.add
-            )
+            nc.vector.tensor_scalar_mul(out=shift[:], in0=row_max[:], scalar1=-SCALE)
             if mt == 0:
                 row_sum[i] = ring.tile([P, ROW_TILES], F32, name="row_sum")
             if mt % 2 == 0:
@@ -193,11 +189,17 @@ def tile_multiheadselfattention2d_pa_kernel(tc, vh, zh, r_pos, x, w_q, out):
                         in_=e_rows[i, half][:, a, t * P : (t + 1) * P],
                         identity=ident_bf[:],
                     )
+            e_planes = stage.tile([P, 2, PACK, P], BF16, name="e_planes")
+            nc.scalar.copy(out=e_planes[:], in_=eT_ps[:])
             if half == 0:
                 e_grouped[i] = stage.tile([P, ROW_TILES, P, PACK], BF16, name="e_grouped", align_bytes=64)
-            nc.scalar.copy(
+            nc.gpsimd.tensor_scalar(
                 out=e_grouped[i][:, 2 * half : 2 * half + 2],
-                in_=eT_ps[:].rearrange("p a t m -> p a m t"),
+                in0=e_planes[:].rearrange("p a t m -> p a m t"),
+                scalar1=1.0,
+                scalar2=0.0,
+                op0=ALU.mult,
+                op1=ALU.add,
             )
 
         def quantise_e(i):
@@ -242,44 +244,53 @@ def tile_multiheadselfattention2d_pa_kernel(tc, vh, zh, r_pos, x, w_q, out):
                     out=oT_ps[:, mt * P : (mt + 1) * P], in_=o_sb[i][:, mt, :], identity=ident_f32[:]
                 )
             out_sb = ring.tile([P, PIX], F32, name="out_sb")
-            nc.vector.tensor_copy(out=out_sb[:], in_=oT_ps[:])
+            if i % 2 == 0:
+                nc.vector.tensor_copy(out=out_sb[:], in_=oT_ps[:])
+            else:
+                nc.scalar.copy(out=out_sb[:], in_=oT_ps[:])
             nc.sync.dma_start(
                 out=out[b, hd * DH : (hd + 1) * DH].rearrange("c h w -> c (h w)"), in_=out_sb[:]
             )
 
-        for i in range(UNITS + 2):
-            scoring = i < UNITS
-            if scoring:
+        def live(u):
+            return 0 <= u < UNITS
+
+        X_ROUND = {0: 0, HEADS - 2: 1}
+
+        for i in range(UNITS + 3):
+            if live(i):
                 scores_and_exp(i, 0)
-            if 1 <= i <= UNITS:
-                project_values(i - 1)
-            if i >= 2:
-                attend(i - 2)
-            if i in (0, HEADS - 1):
-                regroup_x(i // (HEADS - 1), 0)
+            if live(i - 1):
+                transpose_e(i - 1, 0)
+            if live(i - 2):
+                quantise_e(i - 2)
+            if 1 <= i <= HEADS:
+                quantise_w(i - 1)
 
-            if scoring:
+            if live(i):
                 scores_and_exp(i, 1)
-            if 1 <= i <= UNITS:
+            if live(i - 1):
                 transpose_e(i - 1, 1)
-                quantise_q(i - 1)
-            if i in (0, HEADS - 1):
-                regroup_x(i // (HEADS - 1), 1)
-                quantise_x(i // (HEADS - 1), 0)
+            if i in X_ROUND:
+                regroup_x(X_ROUND[i], 0)
 
-            if scoring:
+            if live(i):
                 scores_and_exp(i, 2)
+            if live(i - 2):
+                attend(i - 2)
+            if live(i - 1):
+                project_values(i - 1)
+            if i in X_ROUND:
+                regroup_x(X_ROUND[i], 1)
+                quantise_x(X_ROUND[i], 0)
+
+            if live(i):
+                scores_and_exp(i, 3)
+            if live(i - 3):
+                store_unit(i - 3)
             if i < HEADS:
                 transpose_w(i)
-            if i >= 2:
-                store_unit(i - 2)
-            if 1 <= i <= UNITS:
-                quantise_e(i - 1)
-            if i in (0, HEADS - 1):
-                quantise_x(i // (HEADS - 1), 1)
-
-            if scoring:
-                scores_and_exp(i, 3)
-                transpose_e(i, 0)
-            if i < HEADS:
-                quantise_w(i)
+            if live(i - 1):
+                quantise_q(i - 1)
+            if i in X_ROUND:
+                quantise_x(X_ROUND[i], 1)

@@ -48,11 +48,11 @@ def tile_multiheadselfattention2d_pa_kernel(tc, vh, zh, r_pos, x, w_q, out):
                 r_sb[hd] = inputs.tile([P, PIX], BF16, name="r_sb%d" % hd)
                 nc.sync.dma_start(out=r_sb[hd][:], in_=r_pos[hd])
 
-        def load_x(b):
-            x_sb[b] = inputs.tile([P, K_PASSES, PACK, PIX], BF16, name="x_sb%d" % b)
+        def load_x(b, g):
+            x_sb[b, g] = inputs.tile([P, PACK, PIX], BF16, name="x_sb%d_%d" % (b, g))
             nc.sync.dma_start(
-                out=x_sb[b][:].rearrange("q g (u e) n -> q (g u) (e n)", e=2),
-                in_=x[b].rearrange("(g u q e) h w -> q (g u) (e h w)", g=K_PASSES, u=2, e=2),
+                out=x_sb[b, g][:].rearrange("q (u e) n -> q u (e n)", e=2),
+                in_=x[b, g * P * PACK : (g + 1) * P * PACK].rearrange("(u q e) h w -> q u (e h w)", u=2, e=2),
             )
 
         def load_w(hd):
@@ -60,14 +60,14 @@ def tile_multiheadselfattention2d_pa_kernel(tc, vh, zh, r_pos, x, w_q, out):
             nc.sync.dma_start(out=w_sb[hd][:], in_=w_q[hd * DH : (hd + 1) * DH, :])
 
         load_unit(0)
-        load_unit(1)
-        load_x(0)
         load_w(0)
-        load_w(1)
-        for hd in range(2, HEADS):
+        load_x(0, 0)
+        load_x(0, 1)
+        for hd in range(1, HEADS):
             load_unit(hd)
             load_w(hd)
-        load_x(1)
+        load_x(1, 0)
+        load_x(1, 1)
         for i in range(HEADS, UNITS):
             load_unit(i)
 
@@ -88,7 +88,7 @@ def tile_multiheadselfattention2d_pa_kernel(tc, vh, zh, r_pos, x, w_q, out):
             grouped = stage.tile([P, PIX, PACK], BF16, name="x_grouped", align_bytes=64)
             nc.vector.tensor_copy(
                 out=grouped[:].rearrange("q (c i) t -> q c t i", i=4),
-                in_=x_sb[b][:, g].rearrange("q t (c i) -> q c t i", i=4),
+                in_=x_sb[b, g][:].rearrange("q t (c i) -> q c t i", i=4),
             )
             x_grouped[b, g] = grouped
 
@@ -153,14 +153,18 @@ def tile_multiheadselfattention2d_pa_kernel(tc, vh, zh, r_pos, x, w_q, out):
                 in_=q_grouped[i][:].rearrange("p d t -> p (d t)"),
             )
 
-        e_rows, row_sum = {}, {}
+        s_banks, e_rows, row_sum = {}, {}, {}
 
-        def scores_and_exp(i, mt):
+        def scores(i, mt):
             hd = i % HEADS
             queries = slice(mt * P, (mt + 1) * P)
             s_ps = psum_s.tile([P, PIX], F32, name="s_ps")
             nc.tensor.matmul(out=s_ps[:], lhsT=vh_sb[i][:, queries], rhs=zh_sb[i][:], start=True, stop=False)
             nc.tensor.matmul(out=s_ps[:], lhsT=vh_sb[i][:, queries], rhs=r_sb[hd][:], start=False, stop=True)
+            s_banks[i, mt] = s_ps
+
+        def exp_rows(i, mt):
+            s_ps = s_banks[i, mt]
             row_max = ring.tile([P, 1], F32, name="row_max")
             nc.vector.reduce_max(out=row_max[:], in_=s_ps[:], axis=AXIS.X)
             shift = ring.tile([P, 1], F32, name="shift")
@@ -211,12 +215,14 @@ def tile_multiheadselfattention2d_pa_kernel(tc, vh, zh, r_pos, x, w_q, out):
                 in_=e_grouped[i][:].rearrange("p a m t -> p (a m t)"),
             )
 
-        o_sb = {}
+        inv_sums, o_banks, o_sb, oT_banks = {}, {}, {}, {}
 
         def attend(i):
             inv_sum = ring.tile([P, ROW_TILES], F32, name="inv_sum")
             nc.vector.reciprocal(out=inv_sum[:], in_=row_sum[i][:])
+            inv_sums[i] = inv_sum
             o_ps = psum_m.tile([P, ROW_TILES, DH], F32, name="o_ps", tag="misc")
+            o_banks[i] = o_ps
             for mt in range(ROW_TILES):
                 queries = slice(mt * P, (mt + 1) * P)
                 nc.tensor.matmul_mx(
@@ -228,21 +234,27 @@ def tile_multiheadselfattention2d_pa_kernel(tc, vh, zh, r_pos, x, w_q, out):
                     start=True,
                     stop=True,
                 )
+
+        def normalise(i):
             o_sb[i] = stage.tile([P, ROW_TILES, DH], F32, name="o_sb")
             nc.vector.tensor_tensor(
                 out=o_sb[i][:],
-                in0=o_ps[:],
-                in1=inv_sum[:].unsqueeze(2).to_broadcast([P, ROW_TILES, DH]),
+                in0=o_banks[i][:],
+                in1=inv_sums[i][:].unsqueeze(2).to_broadcast([P, ROW_TILES, DH]),
                 op=ALU.mult,
             )
 
-        def store_unit(i):
-            b, hd = divmod(i, HEADS)
+        def transpose_o(i):
             oT_ps = psum_m.tile([P, PIX], F32, name="oT_ps", tag="misc")
             for mt in range(ROW_TILES):
                 nc.tensor.transpose(
                     out=oT_ps[:, mt * P : (mt + 1) * P], in_=o_sb[i][:, mt, :], identity=ident_f32[:]
                 )
+            oT_banks[i] = oT_ps
+
+        def store_unit(i):
+            b, hd = divmod(i, HEADS)
+            oT_ps = oT_banks[i]
             out_sb = ring.tile([P, PIX], F32, name="out_sb")
             if i % 2 == 0:
                 nc.vector.tensor_copy(out=out_sb[:], in_=oT_ps[:])
@@ -257,40 +269,53 @@ def tile_multiheadselfattention2d_pa_kernel(tc, vh, zh, r_pos, x, w_q, out):
 
         X_ROUND = {0: 0, HEADS - 2: 1}
 
-        for i in range(UNITS + 3):
-            if live(i):
-                scores_and_exp(i, 0)
-            if live(i - 1):
-                transpose_e(i - 1, 0)
-            if live(i - 2):
-                quantise_e(i - 2)
-            if 1 <= i <= HEADS:
-                quantise_w(i - 1)
+        with tc.manual_schedule():
+            for i in range(UNITS + 3):
+                if live(i):
+                    scores(i, 0)
+                if live(i - 1):
+                    transpose_e(i - 1, 0)
+                if live(i):
+                    exp_rows(i, 0)
+                if i - 1 in X_ROUND:
+                    quantise_x(X_ROUND[i - 1], 1)
+                if 1 <= i <= HEADS:
+                    quantise_w(i - 1)
+                if live(i - 2):
+                    quantise_e(i - 2)
 
-            if live(i):
-                scores_and_exp(i, 1)
-            if live(i - 1):
-                transpose_e(i - 1, 1)
-            if i in X_ROUND:
-                regroup_x(X_ROUND[i], 0)
+                if live(i):
+                    scores(i, 1)
+                if live(i - 1):
+                    transpose_e(i - 1, 1)
+                if live(i):
+                    exp_rows(i, 1)
 
-            if live(i):
-                scores_and_exp(i, 2)
-            if live(i - 2):
-                attend(i - 2)
-            if live(i - 1):
-                project_values(i - 1)
-            if i in X_ROUND:
-                regroup_x(X_ROUND[i], 1)
-                quantise_x(X_ROUND[i], 0)
+                if live(i):
+                    scores(i, 2)
+                if live(i - 1):
+                    project_values(i - 1)
+                if live(i - 2):
+                    attend(i - 2)
+                if live(i):
+                    exp_rows(i, 2)
+                if i in X_ROUND:
+                    regroup_x(X_ROUND[i], 0)
+                if live(i - 2):
+                    normalise(i - 2)
 
-            if live(i):
-                scores_and_exp(i, 3)
-            if live(i - 3):
-                store_unit(i - 3)
-            if i < HEADS:
-                transpose_w(i)
-            if live(i - 1):
-                quantise_q(i - 1)
-            if i in X_ROUND:
-                quantise_x(X_ROUND[i], 1)
+                if live(i):
+                    scores(i, 3)
+                if i < HEADS:
+                    transpose_w(i)
+                if live(i - 3):
+                    transpose_o(i - 3)
+                if live(i):
+                    exp_rows(i, 3)
+                if i in X_ROUND:
+                    quantise_x(X_ROUND[i], 0)
+                    regroup_x(X_ROUND[i], 1)
+                if live(i - 1):
+                    quantise_q(i - 1)
+                if live(i - 3):
+                    store_unit(i - 3)

@@ -10,7 +10,6 @@ U8 = mybir.dt.uint8
 FP8X4 = mybir.dt.float8_e4m3fn_x4
 ACT = mybir.ActivationFunctionType
 ALU = mybir.AluOpType
-AXIS = mybir.AxisListType
 
 P = 128
 PACK = 4
@@ -71,8 +70,6 @@ def tile_multiheadselfattention2d_pa_kernel(tc, vh, zh, r_pos, x, w_q, out):
         for i in range(HEADS, UNITS):
             load_unit(i)
 
-        ident_bf = consts.tile([P, P], BF16)
-        make_identity(nc, ident_bf[:])
         ident_f32 = consts.tile([P, P], F32)
         make_identity(nc, ident_f32[:])
         warm = consts.tile([P, 1], F32)
@@ -86,10 +83,12 @@ def tile_multiheadselfattention2d_pa_kernel(tc, vh, zh, r_pos, x, w_q, out):
 
         def regroup_x(b, g):
             grouped = stage.tile([P, PIX, PACK], BF16, name="x_grouped", align_bytes=64)
-            nc.vector.tensor_copy(
-                out=grouped[:].rearrange("q (c i) t -> q c t i", i=4),
-                in_=x_sb[b, g][:].rearrange("q t (c i) -> q c t i", i=4),
-            )
+            for u2 in range(2):
+                cols = slice(2 * u2 * P, 2 * (u2 + 1) * P)
+                nc.vector.tensor_copy(
+                    out=grouped[:, cols, :].rearrange("q (e2 q2) t -> q e2 q2 t", e2=2),
+                    in_=x_sb[b, g][:, :, cols].rearrange("q t (q2 e2) -> q e2 q2 t", e2=2),
+                )
             x_grouped[b, g] = grouped
 
         def quantise_x(b, g):
@@ -153,57 +152,55 @@ def tile_multiheadselfattention2d_pa_kernel(tc, vh, zh, r_pos, x, w_q, out):
                 in_=q_grouped[i][:].rearrange("p d t -> p (d t)"),
             )
 
-        s_banks, e_rows, row_sum = {}, {}, {}
+        e_rows, row_sum = {}, {}
 
-        def scores(i, mt):
+        def scores_and_exp(i, mt):
             hd = i % HEADS
             queries = slice(mt * P, (mt + 1) * P)
             s_ps = psum_s.tile([P, PIX], F32, name="s_ps")
             nc.tensor.matmul(out=s_ps[:], lhsT=vh_sb[i][:, queries], rhs=zh_sb[i][:], start=True, stop=False)
             nc.tensor.matmul(out=s_ps[:], lhsT=vh_sb[i][:, queries], rhs=r_sb[hd][:], start=False, stop=True)
-            s_banks[i, mt] = s_ps
-
-        def exp_rows(i, mt):
-            s_ps = s_banks[i, mt]
-            row_max = ring.tile([P, 1], F32, name="row_max")
-            nc.vector.reduce_max(out=row_max[:], in_=s_ps[:], axis=AXIS.X)
+            neg_scaled = ring.tile([P, PIX], F32, name="neg_scaled")
             shift = ring.tile([P, 1], F32, name="shift")
-            nc.vector.tensor_scalar_mul(out=shift[:], in0=row_max[:], scalar1=-SCALE)
+            nc.vector.tensor_scalar(
+                out=neg_scaled[:],
+                in0=s_ps[:],
+                scalar1=-SCALE,
+                scalar2=None,
+                op0=ALU.mult,
+                op1=ALU.min,
+                accum_out=shift[:],
+            )
             if mt == 0:
                 row_sum[i] = ring.tile([P, ROW_TILES], F32, name="row_sum")
             if mt % 2 == 0:
                 e_rows[i, mt // 2] = ring.tile([P, 2, PIX], BF16, name="e_rows")
             nc.scalar.activation(
                 out=e_rows[i, mt // 2][:, mt % 2, :],
-                in_=s_ps[:],
+                in_=neg_scaled[:],
                 func=ACT.Exp,
                 bias=shift[:],
-                scale=SCALE,
+                scale=-1.0,
                 accum_out=row_sum[i][:, mt : mt + 1],
             )
 
         e_grouped, e_codes, e_scales = {}, {}, {}
 
         def transpose_e(i, half):
-            eT_ps = psum_e.tile([P, 2, PACK, P], BF16, name="eT_ps")
+            e_words = e_rows[i, half][:].bitcast(F32)
+            eT_ps = psum_e.tile([P, 2, 2 * P], F32, name="eT_ps")
             for a in range(2):
-                for t in range(PACK):
+                for u in range(2):
                     nc.tensor.transpose(
-                        out=eT_ps[:, a, t, :],
-                        in_=e_rows[i, half][:, a, t * P : (t + 1) * P],
-                        identity=ident_bf[:],
+                        out=eT_ps[:, u, a * P : (a + 1) * P],
+                        in_=e_words[:, a, u * P : (u + 1) * P],
+                        identity=ident_f32[:],
                     )
-            e_planes = stage.tile([P, 2, PACK, P], BF16, name="e_planes")
-            nc.scalar.copy(out=e_planes[:], in_=eT_ps[:])
             if half == 0:
-                e_grouped[i] = stage.tile([P, ROW_TILES, P, PACK], BF16, name="e_grouped", align_bytes=64)
-            nc.gpsimd.tensor_scalar(
-                out=e_grouped[i][:, 2 * half : 2 * half + 2],
-                in0=e_planes[:].rearrange("p a t m -> p a m t"),
-                scalar1=1.0,
-                scalar2=0.0,
-                op0=ALU.mult,
-                op1=ALU.add,
+                e_grouped[i] = stage.tile([P, PIX, PACK], BF16, name="e_grouped", align_bytes=64)
+            nc.scalar.copy(
+                out=e_grouped[i][:, 2 * half * P : 2 * (half + 1) * P, :].bitcast(F32),
+                in_=eT_ps[:].rearrange("q u m -> q m u"),
             )
 
         def quantise_e(i):
@@ -212,17 +209,15 @@ def tile_multiheadselfattention2d_pa_kernel(tc, vh, zh, r_pos, x, w_q, out):
             nc.vector.quantize_mx(
                 out=e_codes[i][:].bitcast(FP8X4),
                 scales=e_scales[i][:],
-                in_=e_grouped[i][:].rearrange("p a m t -> p (a m t)"),
+                in_=e_grouped[i][:].rearrange("p m t -> p (m t)"),
             )
 
-        inv_sums, o_banks, o_sb, oT_banks = {}, {}, {}, {}
+        o_sb = {}
 
         def attend(i):
             inv_sum = ring.tile([P, ROW_TILES], F32, name="inv_sum")
             nc.vector.reciprocal(out=inv_sum[:], in_=row_sum[i][:])
-            inv_sums[i] = inv_sum
             o_ps = psum_m.tile([P, ROW_TILES, DH], F32, name="o_ps", tag="misc")
-            o_banks[i] = o_ps
             for mt in range(ROW_TILES):
                 queries = slice(mt * P, (mt + 1) * P)
                 nc.tensor.matmul_mx(
@@ -234,27 +229,21 @@ def tile_multiheadselfattention2d_pa_kernel(tc, vh, zh, r_pos, x, w_q, out):
                     start=True,
                     stop=True,
                 )
-
-        def normalise(i):
             o_sb[i] = stage.tile([P, ROW_TILES, DH], F32, name="o_sb")
             nc.vector.tensor_tensor(
                 out=o_sb[i][:],
-                in0=o_banks[i][:],
-                in1=inv_sums[i][:].unsqueeze(2).to_broadcast([P, ROW_TILES, DH]),
+                in0=o_ps[:],
+                in1=inv_sum[:].unsqueeze(2).to_broadcast([P, ROW_TILES, DH]),
                 op=ALU.mult,
             )
 
-        def transpose_o(i):
+        def store_unit(i):
+            b, hd = divmod(i, HEADS)
             oT_ps = psum_m.tile([P, PIX], F32, name="oT_ps", tag="misc")
             for mt in range(ROW_TILES):
                 nc.tensor.transpose(
                     out=oT_ps[:, mt * P : (mt + 1) * P], in_=o_sb[i][:, mt, :], identity=ident_f32[:]
                 )
-            oT_banks[i] = oT_ps
-
-        def store_unit(i):
-            b, hd = divmod(i, HEADS)
-            oT_ps = oT_banks[i]
             out_sb = ring.tile([P, PIX], F32, name="out_sb")
             if i % 2 == 0:
                 nc.vector.tensor_copy(out=out_sb[:], in_=oT_ps[:])
@@ -269,53 +258,40 @@ def tile_multiheadselfattention2d_pa_kernel(tc, vh, zh, r_pos, x, w_q, out):
 
         X_ROUND = {0: 0, HEADS - 2: 1}
 
-        with tc.manual_schedule():
-            for i in range(UNITS + 3):
-                if live(i):
-                    scores(i, 0)
-                if live(i - 1):
-                    transpose_e(i - 1, 0)
-                if live(i):
-                    exp_rows(i, 0)
-                if i - 1 in X_ROUND:
-                    quantise_x(X_ROUND[i - 1], 1)
-                if 1 <= i <= HEADS:
-                    quantise_w(i - 1)
-                if live(i - 2):
-                    quantise_e(i - 2)
+        for i in range(UNITS + 3):
+            if live(i):
+                scores_and_exp(i, 0)
+            if live(i - 1):
+                transpose_e(i - 1, 0)
+            if live(i - 2):
+                quantise_e(i - 2)
+            if 1 <= i <= HEADS:
+                quantise_w(i - 1)
 
-                if live(i):
-                    scores(i, 1)
-                if live(i - 1):
-                    transpose_e(i - 1, 1)
-                if live(i):
-                    exp_rows(i, 1)
+            if live(i):
+                scores_and_exp(i, 1)
+            if live(i - 1):
+                transpose_e(i - 1, 1)
+            if i in X_ROUND:
+                regroup_x(X_ROUND[i], 0)
 
-                if live(i):
-                    scores(i, 2)
-                if live(i - 1):
-                    project_values(i - 1)
-                if live(i - 2):
-                    attend(i - 2)
-                if live(i):
-                    exp_rows(i, 2)
-                if i in X_ROUND:
-                    regroup_x(X_ROUND[i], 0)
-                if live(i - 2):
-                    normalise(i - 2)
+            if live(i):
+                scores_and_exp(i, 2)
+            if live(i - 2):
+                attend(i - 2)
+            if live(i - 1):
+                project_values(i - 1)
+            if i in X_ROUND:
+                regroup_x(X_ROUND[i], 1)
+                quantise_x(X_ROUND[i], 0)
 
-                if live(i):
-                    scores(i, 3)
-                if i < HEADS:
-                    transpose_w(i)
-                if live(i - 3):
-                    transpose_o(i - 3)
-                if live(i):
-                    exp_rows(i, 3)
-                if i in X_ROUND:
-                    quantise_x(X_ROUND[i], 0)
-                    regroup_x(X_ROUND[i], 1)
-                if live(i - 1):
-                    quantise_q(i - 1)
-                if live(i - 3):
-                    store_unit(i - 3)
+            if live(i):
+                scores_and_exp(i, 3)
+            if live(i - 3):
+                store_unit(i - 3)
+            if i < HEADS:
+                transpose_w(i)
+            if live(i - 1):
+                quantise_q(i - 1)
+            if i in X_ROUND:
+                quantise_x(X_ROUND[i], 1)

@@ -152,14 +152,18 @@ def tile_multiheadselfattention2d_pa_kernel(tc, vh, zh, r_pos, x, w_q, out):
                 in_=q_grouped[i][:].rearrange("p d t -> p (d t)"),
             )
 
-        e_rows, row_sum = {}, {}
+        s_banks, e_rows, row_sum = {}, {}, {}
 
-        def scores_and_exp(i, mt):
+        def scores(i, mt):
             hd = i % HEADS
             queries = slice(mt * P, (mt + 1) * P)
             s_ps = psum_s.tile([P, PIX], F32, name="s_ps")
             nc.tensor.matmul(out=s_ps[:], lhsT=vh_sb[i][:, queries], rhs=zh_sb[i][:], start=True, stop=False)
             nc.tensor.matmul(out=s_ps[:], lhsT=vh_sb[i][:, queries], rhs=r_sb[hd][:], start=False, stop=True)
+            s_banks[i, mt] = s_ps
+
+        def exp_rows(i, mt):
+            s_ps = s_banks[i, mt]
             neg_scaled = ring.tile([P, PIX], F32, name="neg_scaled")
             shift = ring.tile([P, 1], F32, name="shift")
             nc.vector.tensor_scalar(
@@ -212,12 +216,14 @@ def tile_multiheadselfattention2d_pa_kernel(tc, vh, zh, r_pos, x, w_q, out):
                 in_=e_grouped[i][:].rearrange("p m t -> p (m t)"),
             )
 
-        o_sb = {}
+        inv_sums, o_banks, o_sb, oT_banks = {}, {}, {}, {}
 
         def attend(i):
             inv_sum = ring.tile([P, ROW_TILES], F32, name="inv_sum")
             nc.vector.reciprocal(out=inv_sum[:], in_=row_sum[i][:])
+            inv_sums[i] = inv_sum
             o_ps = psum_m.tile([P, ROW_TILES, DH], F32, name="o_ps", tag="misc")
+            o_banks[i] = o_ps
             for mt in range(ROW_TILES):
                 queries = slice(mt * P, (mt + 1) * P)
                 nc.tensor.matmul_mx(
@@ -229,21 +235,27 @@ def tile_multiheadselfattention2d_pa_kernel(tc, vh, zh, r_pos, x, w_q, out):
                     start=True,
                     stop=True,
                 )
+
+        def normalise(i):
             o_sb[i] = stage.tile([P, ROW_TILES, DH], F32, name="o_sb")
             nc.vector.tensor_tensor(
                 out=o_sb[i][:],
-                in0=o_ps[:],
-                in1=inv_sum[:].unsqueeze(2).to_broadcast([P, ROW_TILES, DH]),
+                in0=o_banks[i][:],
+                in1=inv_sums[i][:].unsqueeze(2).to_broadcast([P, ROW_TILES, DH]),
                 op=ALU.mult,
             )
 
-        def store_unit(i):
-            b, hd = divmod(i, HEADS)
+        def transpose_o(i):
             oT_ps = psum_m.tile([P, PIX], F32, name="oT_ps", tag="misc")
             for mt in range(ROW_TILES):
                 nc.tensor.transpose(
                     out=oT_ps[:, mt * P : (mt + 1) * P], in_=o_sb[i][:, mt, :], identity=ident_f32[:]
                 )
+            oT_banks[i] = oT_ps
+
+        def store_unit(i):
+            b, hd = divmod(i, HEADS)
+            oT_ps = oT_banks[i]
             out_sb = ring.tile([P, PIX], F32, name="out_sb")
             if i % 2 == 0:
                 nc.vector.tensor_copy(out=out_sb[:], in_=oT_ps[:])
@@ -258,40 +270,53 @@ def tile_multiheadselfattention2d_pa_kernel(tc, vh, zh, r_pos, x, w_q, out):
 
         X_ROUND = {0: 0, HEADS - 2: 1}
 
-        for i in range(UNITS + 3):
-            if live(i):
-                scores_and_exp(i, 0)
-            if live(i - 1):
-                transpose_e(i - 1, 0)
-            if live(i - 2):
-                quantise_e(i - 2)
-            if 1 <= i <= HEADS:
-                quantise_w(i - 1)
+        with tc.manual_schedule():
+            for i in range(UNITS + 3):
+                if live(i):
+                    scores(i, 0)
+                if live(i - 1):
+                    transpose_e(i - 1, 0)
+                if live(i):
+                    exp_rows(i, 0)
+                if i - 1 in X_ROUND:
+                    quantise_x(X_ROUND[i - 1], 1)
+                if 1 <= i <= HEADS:
+                    quantise_w(i - 1)
+                if live(i - 2):
+                    quantise_e(i - 2)
 
-            if live(i):
-                scores_and_exp(i, 1)
-            if live(i - 1):
-                transpose_e(i - 1, 1)
-            if i in X_ROUND:
-                regroup_x(X_ROUND[i], 0)
+                if live(i):
+                    scores(i, 1)
+                if live(i - 1):
+                    transpose_e(i - 1, 1)
+                if live(i):
+                    exp_rows(i, 1)
 
-            if live(i):
-                scores_and_exp(i, 2)
-            if live(i - 2):
-                attend(i - 2)
-            if live(i - 1):
-                project_values(i - 1)
-            if i in X_ROUND:
-                regroup_x(X_ROUND[i], 1)
-                quantise_x(X_ROUND[i], 0)
+                if live(i):
+                    scores(i, 2)
+                if live(i - 1):
+                    project_values(i - 1)
+                if live(i - 2):
+                    attend(i - 2)
+                if live(i):
+                    exp_rows(i, 2)
+                if i in X_ROUND:
+                    regroup_x(X_ROUND[i], 0)
+                if live(i - 2):
+                    normalise(i - 2)
 
-            if live(i):
-                scores_and_exp(i, 3)
-            if live(i - 3):
-                store_unit(i - 3)
-            if i < HEADS:
-                transpose_w(i)
-            if live(i - 1):
-                quantise_q(i - 1)
-            if i in X_ROUND:
-                quantise_x(X_ROUND[i], 1)
+                if live(i):
+                    scores(i, 3)
+                if i < HEADS:
+                    transpose_w(i)
+                if live(i - 3):
+                    transpose_o(i - 3)
+                if live(i):
+                    exp_rows(i, 3)
+                if i in X_ROUND:
+                    quantise_x(X_ROUND[i], 0)
+                    regroup_x(X_ROUND[i], 1)
+                if live(i - 1):
+                    quantise_q(i - 1)
+                if live(i - 3):
+                    store_unit(i - 3)

@@ -156,7 +156,7 @@ def tile_multiheadselfattention2d_pa_kernel(tc, vh, zh, r_pos, x, w_q, out):
 
         def scores(i, mt):
             hd = i % HEADS
-            queries = slice(mt * P, (mt + 1) * P)
+            queries = slice(mt, PIX, ROW_TILES)
             s_ps = psum_s.tile([P, PIX], F32, name="s_ps")
             nc.tensor.matmul(out=s_ps[:], lhsT=vh_sb[i][:, queries], rhs=zh_sb[i][:], start=True, stop=False)
             nc.tensor.matmul(out=s_ps[:], lhsT=vh_sb[i][:, queries], rhs=r_sb[hd][:], start=False, stop=True)
@@ -175,8 +175,9 @@ def tile_multiheadselfattention2d_pa_kernel(tc, vh, zh, r_pos, x, w_q, out):
                 op1=ALU.min,
                 accum_out=shift[:],
             )
-            if mt == 0:
-                row_sum[i] = ring.tile([P, ROW_TILES], F32, name="row_sum")
+            j, a = divmod(i, 2)
+            if a == 0 and mt == 0:
+                row_sum[j] = ring.tile([P, 2, ROW_TILES], F32, name="row_sum")
             if mt % 2 == 0:
                 e_rows[i, mt // 2] = ring.tile([P, 2, PIX], BF16, name="e_rows")
             nc.scalar.activation(
@@ -185,7 +186,7 @@ def tile_multiheadselfattention2d_pa_kernel(tc, vh, zh, r_pos, x, w_q, out):
                 func=ACT.Exp,
                 bias=shift[:],
                 scale=-1.0,
-                accum_out=row_sum[i][:, mt : mt + 1],
+                accum_out=row_sum[j][:, a, mt : mt + 1],
             )
 
         e_grouped, e_codes, e_scales = {}, {}, {}
@@ -216,51 +217,65 @@ def tile_multiheadselfattention2d_pa_kernel(tc, vh, zh, r_pos, x, w_q, out):
                 in_=e_grouped[i][:].rearrange("p m t -> p (m t)"),
             )
 
-        inv_sums, o_banks, o_sb, oT_banks = {}, {}, {}, {}
+        inv_sums, inv_rows = {}, {}
 
-        def attend(i):
-            inv_sum = ring.tile([P, ROW_TILES], F32, name="inv_sum")
-            nc.vector.reciprocal(out=inv_sum[:], in_=row_sum[i][:])
-            inv_sums[i] = inv_sum
-            o_ps = psum_m.tile([P, ROW_TILES, DH], F32, name="o_ps", tag="misc")
-            o_banks[i] = o_ps
-            for mt in range(ROW_TILES):
-                queries = slice(mt * P, (mt + 1) * P)
-                nc.tensor.matmul_mx(
-                    out=o_ps[:, mt, :],
-                    lhsT=e_codes[i][:, queries].bitcast(FP8X4),
-                    lhsT_scale=e_scales[i][:, queries],
-                    rhs=q_codes[i][:].bitcast(FP8X4),
-                    rhs_scale=q_scales[i][:],
-                    start=True,
-                    stop=True,
-                )
-
-        def normalise(i):
-            o_sb[i] = stage.tile([P, ROW_TILES, DH], F32, name="o_sb")
-            nc.vector.tensor_tensor(
-                out=o_sb[i][:],
-                in0=o_banks[i][:],
-                in1=inv_sums[i][:].unsqueeze(2).to_broadcast([P, ROW_TILES, DH]),
-                op=ALU.mult,
+        def invert_sums(j):
+            inv_sums[j] = ring.tile([P, 2, ROW_TILES], F32, name="inv_sum")
+            nc.vector.reciprocal(
+                out=inv_sums[j][:].rearrange("p a t -> p (a t)"), in_=row_sum[j][:].rearrange("p a t -> p (a t)")
             )
 
-        def transpose_o(i):
-            oT_ps = psum_m.tile([P, PIX], F32, name="oT_ps", tag="misc")
+        def spread_by_dma(j):
+            b, hd = divmod(2 * j, HEADS)
+            rows = out[b, hd * DH : hd * DH + 2].rearrange("c h w -> (c h w)")
+            nc.sync.dma_start(
+                out=rows.rearrange("(p k) -> p k", k=2 * ROW_TILES),
+                in_=inv_sums[j][:].rearrange("p a t -> p (a t)"),
+            )
+            spread = ring.tile([P, P, 2, ROW_TILES], F32, name="spread")
+            nc.sync.dma_start(
+                out=spread[:].rearrange("c p a t -> c (p a t)"), in_=rows.partition_broadcast(P)
+            )
+            for a in range(2):
+                inv_rows[2 * j + a] = spread[:, :, a, :]
+
+        def spread_by_transpose(i):
+            j, a = divmod(i, 2)
+            inv_ps = psum_m.tile([P, ROW_TILES, P], F32, name="inv_ps", tag="misc")
             for mt in range(ROW_TILES):
                 nc.tensor.transpose(
-                    out=oT_ps[:, mt * P : (mt + 1) * P], in_=o_sb[i][:, mt, :], identity=ident_f32[:]
+                    out=inv_ps[:, mt, :],
+                    in_=inv_sums[j][:, a, mt : mt + 1].to_broadcast([P, P]),
+                    identity=ident_f32[:],
                 )
-            oT_banks[i] = oT_ps
+            row = ring.tile([P, ROW_TILES, P], F32, name="inv_row")
+            nc.scalar.copy(out=row[:], in_=inv_ps[:])
+            inv_rows[i] = row[:].rearrange("c t p -> c p t")
 
-        def store_unit(i):
+        o_banks = {}
+
+        def attend(i):
+            o_ps = psum_m.tile([P, PIX], F32, name="o_ps", tag="misc")
+            nc.tensor.matmul_mx(
+                out=o_ps[:],
+                lhsT=q_codes[i][:].bitcast(FP8X4),
+                lhsT_scale=q_scales[i][:],
+                rhs=e_codes[i][:].bitcast(FP8X4),
+                rhs_scale=e_scales[i][:],
+                start=True,
+                stop=True,
+            )
+            o_banks[i] = o_ps
+
+        def finish(i):
             b, hd = divmod(i, HEADS)
-            oT_ps = oT_banks[i]
             out_sb = ring.tile([P, PIX], F32, name="out_sb")
-            if i % 2 == 0:
-                nc.vector.tensor_copy(out=out_sb[:], in_=oT_ps[:])
-            else:
-                nc.scalar.copy(out=out_sb[:], in_=oT_ps[:])
+            nc.vector.tensor_tensor(
+                out=out_sb[:].rearrange("c (p t) -> c p t", t=ROW_TILES),
+                in0=o_banks[i][:].rearrange("c (t p) -> c p t", t=ROW_TILES),
+                in1=inv_rows[i],
+                op=ALU.mult,
+            )
             nc.sync.dma_start(
                 out=out[b, hd * DH : (hd + 1) * DH].rearrange("c h w -> c (h w)"), in_=out_sb[:]
             )
@@ -269,9 +284,10 @@ def tile_multiheadselfattention2d_pa_kernel(tc, vh, zh, r_pos, x, w_q, out):
             return 0 <= u < UNITS
 
         X_ROUND = {0: 0, HEADS - 2: 1}
+        LAST_PAIR = UNITS // 2 - 1
 
         with tc.manual_schedule():
-            for i in range(UNITS + 3):
+            for i in range(UNITS + 2):
                 if live(i):
                     scores(i, 0)
                 if live(i - 1):
@@ -282,6 +298,10 @@ def tile_multiheadselfattention2d_pa_kernel(tc, vh, zh, r_pos, x, w_q, out):
                     quantise_x(X_ROUND[i - 1], 1)
                 if 1 <= i <= HEADS:
                     quantise_w(i - 1)
+                if i % 2 == 0 and 0 <= i // 2 - 1 <= LAST_PAIR:
+                    invert_sums(i // 2 - 1)
+                    if i // 2 - 1 < LAST_PAIR:
+                        spread_by_dma(i // 2 - 1)
                 if live(i - 2):
                     quantise_e(i - 2)
 
@@ -296,21 +316,23 @@ def tile_multiheadselfattention2d_pa_kernel(tc, vh, zh, r_pos, x, w_q, out):
                     scores(i, 2)
                 if live(i - 1):
                     project_values(i - 1)
-                if live(i - 2):
-                    attend(i - 2)
                 if live(i):
                     exp_rows(i, 2)
                 if i in X_ROUND:
                     regroup_x(X_ROUND[i], 0)
-                if live(i - 2):
-                    normalise(i - 2)
 
                 if live(i):
                     scores(i, 3)
+                if live(i - 3) and i < UNITS + 1:
+                    attend(i - 3)
+                if i == UNITS:
+                    spread_by_transpose(UNITS - 2)
+                    attend(UNITS - 2)
+                    spread_by_transpose(UNITS - 1)
+                if i == UNITS + 1:
+                    attend(UNITS - 1)
                 if i < HEADS:
                     transpose_w(i)
-                if live(i - 3):
-                    transpose_o(i - 3)
                 if live(i):
                     exp_rows(i, 3)
                 if i in X_ROUND:
@@ -318,5 +340,9 @@ def tile_multiheadselfattention2d_pa_kernel(tc, vh, zh, r_pos, x, w_q, out):
                     regroup_x(X_ROUND[i], 1)
                 if live(i - 1):
                     quantise_q(i - 1)
-                if live(i - 3):
-                    store_unit(i - 3)
+                if live(i - 3) and i < UNITS + 1:
+                    finish(i - 3)
+                if i == UNITS:
+                    finish(UNITS - 2)
+                if i == UNITS + 1:
+                    finish(UNITS - 1)

@@ -18,6 +18,9 @@ C_IN = 1024
 K_PASSES = C_IN // (P * PACK)
 UNITS = BATCH * HEADS
 ROW_TILES = PIX // P
+LAST_PAIR = UNITS // 2 - 1
+X_PIECE = 256
+LOADS_AHEAD = 4
 SCALE = 1.0 / DH**0.5
 
 FLOPS = 2 * UNITS * PIX * PIX * DH * 3 + 2 * BATCH * HEADS * DH * C_IN * PIX
@@ -62,13 +65,9 @@ def tile_multiheadselfattention2d_pa_kernel(tc, vh, zh, r_pos, x, w_q, out):
         load_w(0)
         load_x(0, 0)
         load_x(0, 1)
-        for hd in range(1, HEADS):
+        for hd in range(1, LOADS_AHEAD):
             load_unit(hd)
             load_w(hd)
-        load_x(1, 0)
-        load_x(1, 1)
-        for i in range(HEADS, UNITS):
-            load_unit(i)
 
         ident_f32 = consts.tile([P, P], F32)
         make_identity(nc, ident_f32[:])
@@ -83,12 +82,19 @@ def tile_multiheadselfattention2d_pa_kernel(tc, vh, zh, r_pos, x, w_q, out):
 
         def regroup_x(b, g):
             grouped = stage.tile([P, PIX, PACK], BF16, name="x_grouped", align_bytes=64)
-            for u2 in range(2):
-                cols = slice(2 * u2 * P, 2 * (u2 + 1) * P)
-                nc.vector.tensor_copy(
-                    out=grouped[:, cols, :].rearrange("q (e2 q2) t -> q e2 q2 t", e2=2),
-                    in_=x_sb[b, g][:, :, cols].rearrange("q t (q2 e2) -> q e2 q2 t", e2=2),
-                )
+            flat = x_sb[b, g][:].rearrange("q t n -> q n t")
+            if (b, g) == (0, 0):
+                nc.vector.tensor_copy(out=grouped[:], in_=flat)
+            else:
+                for c in range(0, PIX, X_PIECE):
+                    nc.gpsimd.tensor_scalar(
+                        out=grouped[:, c : c + X_PIECE, :],
+                        in0=flat[:, c : c + X_PIECE, :],
+                        scalar1=1.0,
+                        scalar2=0.0,
+                        op0=ALU.mult,
+                        op1=ALU.add,
+                    )
             x_grouped[b, g] = grouped
 
         def quantise_x(b, g):
@@ -144,8 +150,8 @@ def tile_multiheadselfattention2d_pa_kernel(tc, vh, zh, r_pos, x, w_q, out):
             q_grouped[i] = grouped
 
         def quantise_q(i):
-            q_codes[i] = ring.tile([P, DH], U32, name="q_codes", align_bytes=64)
-            q_scales[i] = ring.tile([P, DH], U8, name="q_scales", align_bytes=64)
+            q_codes[i] = ring.tile([P, DH], U32, name="q_codes", bufs=6, align_bytes=64)
+            q_scales[i] = ring.tile([P, DH], U8, name="q_scales", bufs=6, align_bytes=64)
             nc.vector.quantize_mx(
                 out=q_codes[i][:].bitcast(FP8X4),
                 scales=q_scales[i][:],
@@ -156,7 +162,10 @@ def tile_multiheadselfattention2d_pa_kernel(tc, vh, zh, r_pos, x, w_q, out):
 
         def scores(i, mt):
             hd = i % HEADS
-            queries = slice(mt, PIX, ROW_TILES)
+            if i // 2 == LAST_PAIR:
+                queries = slice(mt * P, (mt + 1) * P)
+            else:
+                queries = slice(mt, PIX, ROW_TILES)
             s_ps = psum_s.tile([P, PIX], F32, name="s_ps")
             nc.tensor.matmul(out=s_ps[:], lhsT=vh_sb[i][:, queries], rhs=zh_sb[i][:], start=True, stop=False)
             nc.tensor.matmul(out=s_ps[:], lhsT=vh_sb[i][:, queries], rhs=r_sb[hd][:], start=False, stop=True)
@@ -181,8 +190,8 @@ def tile_multiheadselfattention2d_pa_kernel(tc, vh, zh, r_pos, x, w_q, out):
             if mt % 2 == 0:
                 e_rows[i, mt // 2] = ring.tile([P, 2, PIX], BF16, name="e_rows")
             nc.scalar.activation(
-                out=e_rows[i, mt // 2][:, mt % 2, :],
-                in_=neg_scaled[:],
+                out=e_rows[i, mt // 2][:, mt % 2, :].rearrange("m (u q e) -> m u q e", u=2, e=2),
+                in_=neg_scaled[:].rearrange("m (u e q) -> m u q e", u=2, e=2),
                 func=ACT.Exp,
                 bias=shift[:],
                 scale=-1.0,
@@ -208,21 +217,24 @@ def tile_multiheadselfattention2d_pa_kernel(tc, vh, zh, r_pos, x, w_q, out):
                 in_=eT_ps[:].rearrange("q u m -> q m u"),
             )
 
-        def quantise_e(i):
-            e_codes[i] = ring.tile([P, PIX], U32, name="e_codes", align_bytes=64)
-            e_scales[i] = ring.tile([P, PIX], U8, name="e_scales", align_bytes=64)
+        def quantise_e(i, first=0, last=PIX):
+            if first == 0:
+                e_codes[i] = ring.tile([P, PIX], U32, name="e_codes", bufs=6, align_bytes=64)
+                e_scales[i] = ring.tile([P, PIX], U8, name="e_scales", bufs=6, align_bytes=64)
             nc.vector.quantize_mx(
-                out=e_codes[i][:].bitcast(FP8X4),
-                scales=e_scales[i][:],
-                in_=e_grouped[i][:].rearrange("p m t -> p (m t)"),
+                out=e_codes[i][:, first:last].bitcast(FP8X4),
+                scales=e_scales[i][:, first:last],
+                in_=e_grouped[i][:, first:last, :].rearrange("p m t -> p (m t)"),
             )
 
         inv_sums, inv_rows = {}, {}
 
-        def invert_sums(j):
-            inv_sums[j] = ring.tile([P, 2, ROW_TILES], F32, name="inv_sum")
+        def invert_sums(j, first=0, count=2):
+            if first == 0:
+                inv_sums[j] = ring.tile([P, 2, ROW_TILES], F32, name="inv_sum")
             nc.vector.reciprocal(
-                out=inv_sums[j][:].rearrange("p a t -> p (a t)"), in_=row_sum[j][:].rearrange("p a t -> p (a t)")
+                out=inv_sums[j][:, first : first + count, :].rearrange("p a t -> p (a t)"),
+                in_=row_sum[j][:, first : first + count, :].rearrange("p a t -> p (a t)"),
             )
 
         def spread_by_dma(j):
@@ -249,100 +261,150 @@ def tile_multiheadselfattention2d_pa_kernel(tc, vh, zh, r_pos, x, w_q, out):
                     identity=ident_f32[:],
                 )
             row = ring.tile([P, ROW_TILES, P], F32, name="inv_row")
-            nc.scalar.copy(out=row[:], in_=inv_ps[:])
-            inv_rows[i] = row[:].rearrange("c t p -> c p t")
+            if a == 0:
+                nc.scalar.copy(out=row[:], in_=inv_ps[:])
+            else:
+                nc.vector.tensor_copy(out=row[:], in_=inv_ps[:])
+            inv_rows[i] = row
 
         o_banks = {}
 
-        def attend(i):
-            o_ps = psum_m.tile([P, PIX], F32, name="o_ps", tag="misc")
+        def attend(i, first=0, last=PIX):
+            if first == 0:
+                o_banks[i] = psum_m.tile([P, PIX], F32, name="o_ps", tag="misc")
             nc.tensor.matmul_mx(
-                out=o_ps[:],
+                out=o_banks[i][:, first:last],
                 lhsT=q_codes[i][:].bitcast(FP8X4),
                 lhsT_scale=q_scales[i][:],
-                rhs=e_codes[i][:].bitcast(FP8X4),
-                rhs_scale=e_scales[i][:],
+                rhs=e_codes[i][:, first:last].bitcast(FP8X4),
+                rhs_scale=e_scales[i][:, first:last],
                 start=True,
                 stop=True,
             )
-            o_banks[i] = o_ps
+
+        out_sb = {}
 
         def finish(i):
             b, hd = divmod(i, HEADS)
-            out_sb = ring.tile([P, PIX], F32, name="out_sb")
+            out_sb[i] = ring.tile([P, PIX], F32, name="out_sb", bufs=6)
             nc.vector.tensor_tensor(
-                out=out_sb[:].rearrange("c (p t) -> c p t", t=ROW_TILES),
+                out=out_sb[i][:].rearrange("c (p t) -> c p t", t=ROW_TILES),
                 in0=o_banks[i][:].rearrange("c (t p) -> c p t", t=ROW_TILES),
                 in1=inv_rows[i],
                 op=ALU.mult,
             )
             nc.sync.dma_start(
-                out=out[b, hd * DH : (hd + 1) * DH].rearrange("c h w -> c (h w)"), in_=out_sb[:]
+                out=out[b, hd * DH : (hd + 1) * DH].rearrange("c h w -> c (h w)"), in_=out_sb[i][:]
+            )
+
+        def finish_part(i, first, last):
+            b, hd = divmod(i, HEADS)
+            if first == 0:
+                out_sb[i] = ring.tile([P, PIX], F32, name="out_sb", bufs=6)
+            nc.vector.tensor_tensor(
+                out=out_sb[i][:, first:last],
+                in0=o_banks[i][:, first:last],
+                in1=inv_rows[i][:].rearrange("c t p -> c (t p)")[:, first:last],
+                op=ALU.mult,
+            )
+            nc.sync.dma_start(
+                out=out[b, hd * DH : (hd + 1) * DH].rearrange("c h w -> c (h w)")[:, first:last],
+                in_=out_sb[i][:, first:last],
             )
 
         def live(u):
             return 0 <= u < UNITS
 
-        X_ROUND = {0: 0, HEADS - 2: 1}
-        LAST_PAIR = UNITS // 2 - 1
+        HALF = PIX // 2
+        PROJECT = {(2, 0): 0, (2, 2): 1, (3, 0): 2, (3, 2): 3}
+        for u in range(4, UNITS):
+            PROJECT[u, 0] = u
 
         with tc.manual_schedule():
-            for i in range(UNITS + 2):
-                if live(i):
-                    scores(i, 0)
-                if live(i - 1):
-                    transpose_e(i - 1, 0)
-                if live(i):
-                    exp_rows(i, 0)
-                if i - 1 in X_ROUND:
-                    quantise_x(X_ROUND[i - 1], 1)
-                if 1 <= i <= HEADS:
-                    quantise_w(i - 1)
-                if i % 2 == 0 and 0 <= i // 2 - 1 <= LAST_PAIR:
-                    invert_sums(i // 2 - 1)
-                    if i // 2 - 1 < LAST_PAIR:
-                        spread_by_dma(i // 2 - 1)
-                if live(i - 2):
-                    quantise_e(i - 2)
+            for i in range(UNITS):
+                if i + LOADS_AHEAD < UNITS:
+                    load_unit(i + LOADS_AHEAD)
+                if i + LOADS_AHEAD < HEADS:
+                    load_w(i + LOADS_AHEAD)
+                if i < K_PASSES:
+                    load_x(1, i)
+                pair_out = (i - 5) // 2 if i % 2 == 1 and i >= 5 else None
 
-                if live(i):
-                    scores(i, 1)
+                scores(i, 0)
+                if i == 1:
+                    transpose_w(1)
+                if (i, 0) in PROJECT:
+                    project_values(PROJECT[i, 0])
+                if pair_out is not None:
+                    attend(2 * pair_out)
+                exp_rows(i, 0)
+                if i % 2 == 0 and i >= 2:
+                    invert_sums(i // 2 - 1)
+                    spread_by_dma(i // 2 - 1)
+                if i == UNITS - 1:
+                    invert_sums(LAST_PAIR, 0, 1)
+                if (i - 1, 2) in PROJECT:
+                    quantise_q(PROJECT[i - 1, 2])
+                if i == 1:
+                    quantise_x(0, 0)
+                if i in (4, 5):
+                    quantise_x(1, i - 4)
+
+                scores(i, 1)
+                if i == 0:
+                    transpose_w(0)
                 if live(i - 1):
                     transpose_e(i - 1, 1)
-                if live(i):
-                    exp_rows(i, 1)
+                exp_rows(i, 1)
+                if pair_out is not None:
+                    finish(2 * pair_out)
+                if i == 1:
+                    quantise_w(1)
 
-                if live(i):
-                    scores(i, 2)
-                if live(i - 1):
-                    project_values(i - 1)
-                if live(i):
-                    exp_rows(i, 2)
-                if i in X_ROUND:
-                    regroup_x(X_ROUND[i], 0)
-
-                if live(i):
-                    scores(i, 3)
-                if live(i - 3) and i < UNITS + 1:
-                    attend(i - 3)
-                if i == UNITS:
+                scores(i, 2)
+                if 1 <= i < HEADS - 1:
+                    transpose_w(i + 1)
+                if (i, 2) in PROJECT:
+                    project_values(PROJECT[i, 2])
+                if pair_out is not None:
+                    attend(2 * pair_out + 1)
+                if i == UNITS - 1:
                     spread_by_transpose(UNITS - 2)
-                    attend(UNITS - 2)
-                    spread_by_transpose(UNITS - 1)
-                if i == UNITS + 1:
-                    attend(UNITS - 1)
-                if i < HEADS:
-                    transpose_w(i)
-                if live(i):
-                    exp_rows(i, 3)
-                if i in X_ROUND:
-                    quantise_x(X_ROUND[i], 0)
-                    regroup_x(X_ROUND[i], 1)
+                exp_rows(i, 2)
+                if i == 0:
+                    quantise_w(0)
+                    regroup_x(0, 0)
+                    regroup_x(0, 1)
+                if i in (2, 3):
+                    regroup_x(1, i - 2)
+                if i == 1:
+                    quantise_x(0, 1)
+                if (i, 0) in PROJECT:
+                    quantise_q(PROJECT[i, 0])
                 if live(i - 1):
-                    quantise_q(i - 1)
-                if live(i - 3) and i < UNITS + 1:
-                    finish(i - 3)
-                if i == UNITS:
-                    finish(UNITS - 2)
-                if i == UNITS + 1:
-                    finish(UNITS - 1)
+                    quantise_e(i - 1)
+
+                scores(i, 3)
+                transpose_e(i, 0)
+                exp_rows(i, 3)
+                if 1 <= i < HEADS - 1:
+                    quantise_w(i + 1)
+                if pair_out is not None:
+                    finish(2 * pair_out + 1)
+                if i == UNITS - 1:
+                    attend(UNITS - 4)
+                    finish(UNITS - 4)
+
+            attend(UNITS - 3)
+            transpose_e(UNITS - 1, 1)
+            attend(UNITS - 2)
+            quantise_e(UNITS - 1, 0, HALF)
+            finish(UNITS - 3)
+            invert_sums(LAST_PAIR, 1, 1)
+            finish_part(UNITS - 2, 0, PIX)
+            spread_by_transpose(UNITS - 1)
+            quantise_e(UNITS - 1, HALF, PIX)
+            attend(UNITS - 1, 0, HALF)
+            attend(UNITS - 1, HALF, PIX)
+            finish_part(UNITS - 1, 0, HALF)
+            finish_part(UNITS - 1, HALF, PIX)

@@ -162,10 +162,7 @@ def tile_multiheadselfattention2d_pa_kernel(tc, vh, zh, r_pos, x, w_q, out):
 
         def scores(i, mt):
             hd = i % HEADS
-            if i // 2 == LAST_PAIR:
-                queries = slice(mt * P, (mt + 1) * P)
-            else:
-                queries = slice(mt, PIX, ROW_TILES)
+            queries = slice(mt * P, (mt + 1) * P)
             s_ps = psum_s.tile([P, PIX], F32, name="s_ps")
             nc.tensor.matmul(out=s_ps[:], lhsT=vh_sb[i][:, queries], rhs=zh_sb[i][:], start=True, stop=False)
             nc.tensor.matmul(out=s_ps[:], lhsT=vh_sb[i][:, queries], rhs=r_sb[hd][:], start=False, stop=True)
@@ -229,27 +226,33 @@ def tile_multiheadselfattention2d_pa_kernel(tc, vh, zh, r_pos, x, w_q, out):
 
         inv_sums, inv_rows = {}, {}
 
+        inv_tiles = []
+        for k in range(2):
+            inv_tile = consts.tile([P, P], F32, name="inv_tile%d" % k)
+            nc.gpsimd.memset(inv_tile[:], 0.0)
+            inv_tiles.append(inv_tile)
+
         def invert_sums(j, first=0, count=2):
-            if first == 0:
-                inv_sums[j] = ring.tile([P, 2, ROW_TILES], F32, name="inv_sum")
+            cols = slice(first * ROW_TILES, (first + count) * ROW_TILES)
+            inv_sums[j] = inv_tiles[j % 2]
             nc.vector.reciprocal(
-                out=inv_sums[j][:, first : first + count, :].rearrange("p a t -> p (a t)"),
-                in_=row_sum[j][:, first : first + count, :].rearrange("p a t -> p (a t)"),
+                out=inv_sums[j][:, cols], in_=row_sum[j][:].rearrange("p a t -> p (a t)")[:, cols]
             )
 
         def spread_by_dma(j):
+            turned = psum_m.tile([P, P], F32, name="inv_turned", tag="misc")
+            nc.tensor.transpose(out=turned[:], in_=inv_sums[j][:], identity=ident_f32[:])
+            rows_sb = ring.tile([2 * ROW_TILES, P], F32, name="inv_rows_sb")
+            nc.scalar.copy(out=rows_sb[:], in_=turned[: 2 * ROW_TILES, :])
             b, hd = divmod(2 * j, HEADS)
             rows = out[b, hd * DH : hd * DH + 2].rearrange("c h w -> (c h w)")
+            nc.sync.dma_start(out=rows.rearrange("(k p) -> k p", p=P), in_=rows_sb[:])
+            spread = ring.tile([P, 2, PIX], F32, name="spread")
             nc.sync.dma_start(
-                out=rows.rearrange("(p k) -> p k", k=2 * ROW_TILES),
-                in_=inv_sums[j][:].rearrange("p a t -> p (a t)"),
-            )
-            spread = ring.tile([P, P, 2, ROW_TILES], F32, name="spread")
-            nc.sync.dma_start(
-                out=spread[:].rearrange("c p a t -> c (p a t)"), in_=rows.partition_broadcast(P)
+                out=spread[:].rearrange("c a m -> c (a m)"), in_=rows.partition_broadcast(P)
             )
             for a in range(2):
-                inv_rows[2 * j + a] = spread[:, :, a, :]
+                inv_rows[2 * j + a] = spread[:, a, :]
 
         def spread_by_transpose(i):
             j, a = divmod(i, 2)
@@ -257,7 +260,7 @@ def tile_multiheadselfattention2d_pa_kernel(tc, vh, zh, r_pos, x, w_q, out):
             for mt in range(ROW_TILES):
                 nc.tensor.transpose(
                     out=inv_ps[:, mt, :],
-                    in_=inv_sums[j][:, a, mt : mt + 1].to_broadcast([P, P]),
+                    in_=inv_sums[j][:, a * ROW_TILES + mt : a * ROW_TILES + mt + 1].to_broadcast([P, P]),
                     identity=ident_f32[:],
                 )
             row = ring.tile([P, ROW_TILES, P], F32, name="inv_row")
@@ -265,7 +268,7 @@ def tile_multiheadselfattention2d_pa_kernel(tc, vh, zh, r_pos, x, w_q, out):
                 nc.scalar.copy(out=row[:], in_=inv_ps[:])
             else:
                 nc.vector.tensor_copy(out=row[:], in_=inv_ps[:])
-            inv_rows[i] = row
+            inv_rows[i] = row[:].rearrange("c t p -> c (t p)")
 
         o_banks = {}
 
@@ -284,27 +287,14 @@ def tile_multiheadselfattention2d_pa_kernel(tc, vh, zh, r_pos, x, w_q, out):
 
         out_sb = {}
 
-        def finish(i):
-            b, hd = divmod(i, HEADS)
-            out_sb[i] = ring.tile([P, PIX], F32, name="out_sb", bufs=6)
-            nc.vector.tensor_tensor(
-                out=out_sb[i][:].rearrange("c (p t) -> c p t", t=ROW_TILES),
-                in0=o_banks[i][:].rearrange("c (t p) -> c p t", t=ROW_TILES),
-                in1=inv_rows[i],
-                op=ALU.mult,
-            )
-            nc.sync.dma_start(
-                out=out[b, hd * DH : (hd + 1) * DH].rearrange("c h w -> c (h w)"), in_=out_sb[i][:]
-            )
-
-        def finish_part(i, first, last):
+        def finish(i, first=0, last=PIX):
             b, hd = divmod(i, HEADS)
             if first == 0:
                 out_sb[i] = ring.tile([P, PIX], F32, name="out_sb", bufs=6)
             nc.vector.tensor_tensor(
                 out=out_sb[i][:, first:last],
                 in0=o_banks[i][:, first:last],
-                in1=inv_rows[i][:].rearrange("c t p -> c (t p)")[:, first:last],
+                in1=inv_rows[i][:, first:last],
                 op=ALU.mult,
             )
             nc.sync.dma_start(
@@ -338,9 +328,6 @@ def tile_multiheadselfattention2d_pa_kernel(tc, vh, zh, r_pos, x, w_q, out):
                 if pair_out is not None:
                     attend(2 * pair_out)
                 exp_rows(i, 0)
-                if i % 2 == 0 and i >= 2:
-                    invert_sums(i // 2 - 1)
-                    spread_by_dma(i // 2 - 1)
                 if i == UNITS - 1:
                     invert_sums(LAST_PAIR, 0, 1)
                 if (i - 1, 2) in PROJECT:
@@ -356,6 +343,8 @@ def tile_multiheadselfattention2d_pa_kernel(tc, vh, zh, r_pos, x, w_q, out):
                 if live(i - 1):
                     transpose_e(i - 1, 1)
                 exp_rows(i, 1)
+                if i % 2 == 0 and i >= 2:
+                    invert_sums(i // 2 - 1)
                 if pair_out is not None:
                     finish(2 * pair_out)
                 if i == 1:
@@ -370,6 +359,8 @@ def tile_multiheadselfattention2d_pa_kernel(tc, vh, zh, r_pos, x, w_q, out):
                     attend(2 * pair_out + 1)
                 if i == UNITS - 1:
                     spread_by_transpose(UNITS - 2)
+                if i % 2 == 0 and i >= 2:
+                    spread_by_dma(i // 2 - 1)
                 exp_rows(i, 2)
                 if i == 0:
                     quantise_w(0)
@@ -401,10 +392,10 @@ def tile_multiheadselfattention2d_pa_kernel(tc, vh, zh, r_pos, x, w_q, out):
             quantise_e(UNITS - 1, 0, HALF)
             finish(UNITS - 3)
             invert_sums(LAST_PAIR, 1, 1)
-            finish_part(UNITS - 2, 0, PIX)
+            finish(UNITS - 2, 0, PIX)
             spread_by_transpose(UNITS - 1)
             quantise_e(UNITS - 1, HALF, PIX)
             attend(UNITS - 1, 0, HALF)
             attend(UNITS - 1, HALF, PIX)
-            finish_part(UNITS - 1, 0, HALF)
-            finish_part(UNITS - 1, HALF, PIX)
+            finish(UNITS - 1, 0, HALF)
+            finish(UNITS - 1, HALF, PIX)

@@ -106,7 +106,7 @@ def tile_multiheadselfattention2d_pa_kernel(tc, vh, zh, r_pos, x, w_q, out):
 
         w_codes = kept.tile([P, HEADS, K_PASSES, DH], U32, align_bytes=64)
         w_scales = kept.tile([P, HEADS, K_PASSES, DH], U8, align_bytes=64)
-        w_grouped = {}
+        w_banks, w_grouped = {}, {}
 
         def transpose_w(hd):
             w_words = w_sb[hd][:].bitcast(F32)
@@ -117,9 +117,13 @@ def tile_multiheadselfattention2d_pa_kernel(tc, vh, zh, r_pos, x, w_q, out):
                     nc.tensor.transpose(
                         out=wT_ps[:, g, u, :], in_=w_words[:, first : first + P], identity=ident_f32[:]
                     )
-            grouped = stage.tile([P, K_PASSES, DH, PACK], BF16, name="w_grouped", align_bytes=64)
-            nc.scalar.copy(out=grouped[:].bitcast(F32), in_=wT_ps[:].rearrange("q g u c -> q g c u"))
-            w_grouped[hd] = grouped
+            w_banks[hd] = wT_ps
+
+        def copy_w(hd):
+            w_grouped[hd] = stage.tile([P, K_PASSES, DH, PACK], BF16, name="w_grouped", align_bytes=64)
+            nc.scalar.copy(
+                out=w_grouped[hd][:].bitcast(F32), in_=w_banks[hd][:].rearrange("q g u c -> q g c u")
+            )
 
         def quantise_w(hd):
             nc.vector.quantize_mx(
@@ -128,7 +132,7 @@ def tile_multiheadselfattention2d_pa_kernel(tc, vh, zh, r_pos, x, w_q, out):
                 in_=w_grouped[hd][:].rearrange("q g c t -> q (g c t)"),
             )
 
-        q_grouped, q_codes, q_scales = {}, {}, {}
+        q_banks, q_grouped, q_codes, q_scales = {}, {}, {}, {}
 
         def project_values(i):
             b, hd = divmod(i, HEADS)
@@ -145,9 +149,11 @@ def tile_multiheadselfattention2d_pa_kernel(tc, vh, zh, r_pos, x, w_q, out):
                         start=(g == 0),
                         stop=(g == K_PASSES - 1),
                     )
-            grouped = stage.tile([P, DH, PACK], BF16, name="q_grouped", align_bytes=64)
-            nc.scalar.copy(out=grouped[:], in_=qT_ps[:].rearrange("p t d -> p d t"))
-            q_grouped[i] = grouped
+            q_banks[i] = qT_ps
+
+        def copy_q(i):
+            q_grouped[i] = stage.tile([P, DH, PACK], BF16, name="q_grouped", align_bytes=64)
+            nc.scalar.copy(out=q_grouped[i][:], in_=q_banks[i][:].rearrange("p t d -> p d t"))
 
         def quantise_q(i):
             q_codes[i] = ring.tile([P, DH], U32, name="q_codes", bufs=6, align_bytes=64)
@@ -158,7 +164,7 @@ def tile_multiheadselfattention2d_pa_kernel(tc, vh, zh, r_pos, x, w_q, out):
                 in_=q_grouped[i][:].rearrange("p d t -> p (d t)"),
             )
 
-        s_banks, e_rows, row_sum = {}, {}, {}
+        s_banks, scaled, e_rows, row_sum = {}, {}, {}, {}
 
         def scores(i, mt):
             hd = i % HEADS
@@ -168,10 +174,11 @@ def tile_multiheadselfattention2d_pa_kernel(tc, vh, zh, r_pos, x, w_q, out):
             nc.tensor.matmul(out=s_ps[:], lhsT=vh_sb[i][:, queries], rhs=r_sb[hd][:], start=False, stop=True)
             s_banks[i, mt] = s_ps
 
-        def exp_rows(i, mt):
+        def max_rows(i, mt):
             s_ps = s_banks[i, mt]
             neg_scaled = ring.tile([P, PIX], F32, name="neg_scaled")
             shift = ring.tile([P, 1], F32, name="shift")
+            scaled[i, mt] = neg_scaled, shift
             nc.vector.tensor_scalar(
                 out=neg_scaled[:],
                 in0=s_ps[:],
@@ -181,6 +188,9 @@ def tile_multiheadselfattention2d_pa_kernel(tc, vh, zh, r_pos, x, w_q, out):
                 op1=ALU.min,
                 accum_out=shift[:],
             )
+
+        def exp_rows(i, mt):
+            neg_scaled, shift = scaled[i, mt]
             j, a = divmod(i, 2)
             if a == 0 and mt == 0:
                 row_sum[j] = ring.tile([P, 2, ROW_TILES], F32, name="row_sum")
@@ -195,23 +205,25 @@ def tile_multiheadselfattention2d_pa_kernel(tc, vh, zh, r_pos, x, w_q, out):
                 accum_out=row_sum[j][:, a, mt : mt + 1],
             )
 
-        e_grouped, e_codes, e_scales = {}, {}, {}
+        eT_banks, e_grouped, e_codes, e_scales = {}, {}, {}, {}
 
-        def transpose_e(i, half):
-            e_words = e_rows[i, half][:].bitcast(F32)
-            eT_ps = psum_e.tile([P, 2, 2 * P], F32, name="eT_ps")
-            for a in range(2):
+        def transpose_e(i, first, count):
+            eT_ps = psum_e.tile([P, 2, count * P], F32, name="eT_ps")
+            for mt in range(first, first + count):
+                e_words = e_rows[i, mt // 2][:, mt % 2, :].bitcast(F32)
+                cols = slice((mt - first) * P, (mt - first + 1) * P)
                 for u in range(2):
                     nc.tensor.transpose(
-                        out=eT_ps[:, u, a * P : (a + 1) * P],
-                        in_=e_words[:, a, u * P : (u + 1) * P],
-                        identity=ident_f32[:],
+                        out=eT_ps[:, u, cols], in_=e_words[:, u * P : (u + 1) * P], identity=ident_f32[:]
                     )
-            if half == 0:
+            eT_banks[i, first] = eT_ps
+
+        def copy_e(i, first, count):
+            if first == 0:
                 e_grouped[i] = stage.tile([P, PIX, PACK], BF16, name="e_grouped", align_bytes=64)
             nc.scalar.copy(
-                out=e_grouped[i][:, 2 * half * P : 2 * (half + 1) * P, :].bitcast(F32),
-                in_=eT_ps[:].rearrange("q u m -> q m u"),
+                out=e_grouped[i][:, first * P : (first + count) * P, :].bitcast(F32),
+                in_=eT_banks[i, first][:].rearrange("q u m -> q m u"),
             )
 
         def quantise_e(i, first=0, last=PIX):
@@ -224,7 +236,7 @@ def tile_multiheadselfattention2d_pa_kernel(tc, vh, zh, r_pos, x, w_q, out):
                 in_=e_grouped[i][:, first:last, :].rearrange("p m t -> p (m t)"),
             )
 
-        inv_sums, inv_rows = {}, {}
+        inv_sums, inv_banks, row_banks, inv_rows = {}, {}, {}, {}
 
         inv_tiles = []
         for k in range(2):
@@ -232,18 +244,21 @@ def tile_multiheadselfattention2d_pa_kernel(tc, vh, zh, r_pos, x, w_q, out):
             nc.gpsimd.memset(inv_tile[:], 0.0)
             inv_tiles.append(inv_tile)
 
-        def invert_sums(j, first=0, count=2):
-            cols = slice(first * ROW_TILES, (first + count) * ROW_TILES)
+        def invert_sums(j, first=0, count=2 * ROW_TILES):
+            cols = slice(first, first + count)
             inv_sums[j] = inv_tiles[j % 2]
             nc.vector.reciprocal(
                 out=inv_sums[j][:, cols], in_=row_sum[j][:].rearrange("p a t -> p (a t)")[:, cols]
             )
 
-        def spread_by_dma(j):
+        def turn_sums(j):
             turned = psum_m.tile([P, P], F32, name="inv_turned", tag="misc")
             nc.tensor.transpose(out=turned[:], in_=inv_sums[j][:], identity=ident_f32[:])
+            inv_banks[j] = turned
+
+        def spread_by_dma(j):
             rows_sb = ring.tile([2 * ROW_TILES, P], F32, name="inv_rows_sb")
-            nc.scalar.copy(out=rows_sb[:], in_=turned[: 2 * ROW_TILES, :])
+            nc.scalar.copy(out=rows_sb[:], in_=inv_banks[j][: 2 * ROW_TILES, :])
             b, hd = divmod(2 * j, HEADS)
             rows = out[b, hd * DH : hd * DH + 2].rearrange("c h w -> (c h w)")
             nc.sync.dma_start(out=rows.rearrange("(k p) -> k p", p=P), in_=rows_sb[:])
@@ -254,27 +269,31 @@ def tile_multiheadselfattention2d_pa_kernel(tc, vh, zh, r_pos, x, w_q, out):
             for a in range(2):
                 inv_rows[2 * j + a] = spread[:, a, :]
 
-        def spread_by_transpose(i):
+        def spread_by_transpose(i, first=0, count=ROW_TILES):
             j, a = divmod(i, 2)
-            inv_ps = psum_m.tile([P, ROW_TILES, P], F32, name="inv_ps", tag="misc")
-            for mt in range(ROW_TILES):
+            if first == 0:
+                row_banks[i] = psum_m.tile([P, PIX], F32, name="row_ps", tag="misc")
+            for mt in range(first, first + count):
+                col = a * ROW_TILES + mt
                 nc.tensor.transpose(
-                    out=inv_ps[:, mt, :],
-                    in_=inv_sums[j][:, a * ROW_TILES + mt : a * ROW_TILES + mt + 1].to_broadcast([P, P]),
+                    out=row_banks[i][:, mt * P : (mt + 1) * P],
+                    in_=inv_sums[j][:, col : col + 1].to_broadcast([P, P]),
                     identity=ident_f32[:],
                 )
-            row = ring.tile([P, ROW_TILES, P], F32, name="inv_row")
-            if a == 0:
-                nc.scalar.copy(out=row[:], in_=inv_ps[:])
-            else:
-                nc.vector.tensor_copy(out=row[:], in_=inv_ps[:])
-            inv_rows[i] = row[:].rearrange("c t p -> c (t p)")
+
+        def copy_row(i, copy, first=0, count=ROW_TILES):
+            if first == 0:
+                inv_rows[i] = ring.tile([P, PIX], F32, name="inv_row")
+            cols = slice(first * P, (first + count) * P)
+            copy(out=inv_rows[i][:, cols], in_=row_banks[i][:, cols])
 
         o_banks = {}
 
         def attend(i, first=0, last=PIX):
-            if first == 0:
+            if first == 0 and i < UNITS - 3:
                 o_banks[i] = psum_m.tile([P, PIX], F32, name="o_ps", tag="misc")
+            elif first == 0:
+                o_banks[i] = psum_s.tile([P, PIX], F32, name="s_ps")
             nc.tensor.matmul_mx(
                 out=o_banks[i][:, first:last],
                 lhsT=q_codes[i][:].bitcast(FP8X4),
@@ -305,10 +324,15 @@ def tile_multiheadselfattention2d_pa_kernel(tc, vh, zh, r_pos, x, w_q, out):
         def live(u):
             return 0 <= u < UNITS
 
-        HALF = PIX // 2
-        PROJECT = {(2, 0): 0, (2, 2): 1, (3, 0): 2, (3, 2): 3}
-        for u in range(4, UNITS):
-            PROJECT[u, 0] = u
+        LAST = UNITS - 1
+        PROJECT = {}
+        for u in range(UNITS):
+            if u < 6:
+                r = u + 2
+            else:
+                r = max(u, 8 + (u - 6) // 2)
+            PROJECT.setdefault(r, []).append(u)
+        W_ROUND = {0: [0], 1: [1, 2], 2: [3], 3: [4], 4: [5], 5: [6], 6: [7]}
 
         with tc.manual_schedule():
             for i in range(UNITS):
@@ -318,84 +342,92 @@ def tile_multiheadselfattention2d_pa_kernel(tc, vh, zh, r_pos, x, w_q, out):
                     load_w(i + LOADS_AHEAD)
                 if i < K_PASSES:
                     load_x(1, i)
-                pair_out = (i - 5) // 2 if i % 2 == 1 and i >= 5 else None
 
                 scores(i, 0)
-                if i == 1:
-                    transpose_w(1)
-                if (i, 0) in PROJECT:
-                    project_values(PROJECT[i, 0])
-                if pair_out is not None:
-                    attend(2 * pair_out)
-                exp_rows(i, 0)
-                if i == UNITS - 1:
-                    invert_sums(LAST_PAIR, 0, 1)
-                if (i - 1, 2) in PROJECT:
-                    quantise_q(PROJECT[i - 1, 2])
+                if live(i - 1):
+                    transpose_e(i - 1, 0, 2)
+                max_rows(i, 0)
+                if live(i - 2):
+                    quantise_e(i - 2)
                 if i == 1:
                     quantise_x(0, 0)
-                if i in (4, 5):
-                    quantise_x(1, i - 4)
+                if live(i - 1):
+                    copy_e(i - 1, 0, 2)
+                exp_rows(i, 0)
 
                 scores(i, 1)
-                if i == 0:
-                    transpose_w(0)
-                if live(i - 1):
-                    transpose_e(i - 1, 1)
-                exp_rows(i, 1)
+                for u in PROJECT.get(i, []):
+                    project_values(u)
+                max_rows(i, 1)
+                for hd in W_ROUND.get(i - 1, []):
+                    quantise_w(hd)
                 if i % 2 == 0 and i >= 2:
                     invert_sums(i // 2 - 1)
-                if pair_out is not None:
-                    finish(2 * pair_out)
-                if i == 1:
-                    quantise_w(1)
+                if i == LAST:
+                    invert_sums(LAST_PAIR, 0, ROW_TILES)
+                if i in (4, 5):
+                    quantise_x(1, i - 4)
+                for u in PROJECT.get(i, []):
+                    copy_q(u)
+                exp_rows(i, 1)
 
                 scores(i, 2)
-                if 1 <= i < HEADS - 1:
-                    transpose_w(i + 1)
-                if (i, 2) in PROJECT:
-                    project_values(PROJECT[i, 2])
-                if pair_out is not None:
-                    attend(2 * pair_out + 1)
-                if i == UNITS - 1:
-                    spread_by_transpose(UNITS - 2)
+                if live(i - 1):
+                    transpose_e(i - 1, 2, 2)
                 if i % 2 == 0 and i >= 2:
-                    spread_by_dma(i // 2 - 1)
-                exp_rows(i, 2)
+                    turn_sums(i // 2 - 1)
+                if i == LAST:
+                    spread_by_transpose(LAST - 1)
+                max_rows(i, 2)
                 if i == 0:
-                    quantise_w(0)
                     regroup_x(0, 0)
                     regroup_x(0, 1)
                 if i in (2, 3):
                     regroup_x(1, i - 2)
                 if i == 1:
                     quantise_x(0, 1)
-                if (i, 0) in PROJECT:
-                    quantise_q(PROJECT[i, 0])
                 if live(i - 1):
-                    quantise_e(i - 1)
+                    copy_e(i - 1, 2, 2)
+                if i % 2 == 0 and i >= 2:
+                    spread_by_dma(i // 2 - 1)
+                exp_rows(i, 2)
 
                 scores(i, 3)
-                transpose_e(i, 0)
+                if live(i - 4):
+                    attend(i - 4)
+                for hd in W_ROUND.get(i, []):
+                    transpose_w(hd)
+                max_rows(i, 3)
+                for u in PROJECT.get(i, []):
+                    quantise_q(u)
+                for hd in W_ROUND.get(i, []):
+                    copy_w(hd)
+                if i == LAST:
+                    copy_row(LAST - 1, nc.scalar.copy)
                 exp_rows(i, 3)
-                if 1 <= i < HEADS - 1:
-                    quantise_w(i + 1)
-                if pair_out is not None:
-                    finish(2 * pair_out + 1)
-                if i == UNITS - 1:
-                    attend(UNITS - 4)
-                    finish(UNITS - 4)
+                if live(i - 4):
+                    finish(i - 4)
 
-            attend(UNITS - 3)
-            transpose_e(UNITS - 1, 1)
-            attend(UNITS - 2)
-            quantise_e(UNITS - 1, 0, HALF)
-            finish(UNITS - 3)
-            invert_sums(LAST_PAIR, 1, 1)
-            finish(UNITS - 2, 0, PIX)
-            spread_by_transpose(UNITS - 1)
-            quantise_e(UNITS - 1, HALF, PIX)
-            attend(UNITS - 1, 0, HALF)
-            attend(UNITS - 1, HALF, PIX)
-            finish(UNITS - 1, 0, HALF)
-            finish(UNITS - 1, HALF, PIX)
+            transpose_e(LAST, 0, 2)
+            attend(LAST - 3)
+            transpose_e(LAST, 2, 1)
+            quantise_e(LAST - 1)
+            copy_e(LAST, 0, 2)
+            copy_e(LAST, 2, 1)
+            invert_sums(LAST_PAIR, ROW_TILES, ROW_TILES)
+            attend(LAST - 2)
+            attend(LAST - 1)
+            transpose_e(LAST, 3, 1)
+            spread_by_transpose(LAST)
+            copy_e(LAST, 3, 1)
+            copy_row(LAST, nc.scalar.copy)
+            finish(LAST - 1)
+            quantise_e(LAST, 0, 2 * P)
+            quantise_e(LAST, 2 * P, 3 * P)
+            quantise_e(LAST, 3 * P, 4 * P)
+            attend(LAST, 0, 2 * P)
+            attend(LAST, 2 * P, 3 * P)
+            attend(LAST, 3 * P, 4 * P)
+            finish(LAST - 3)
+            finish(LAST)
+            finish(LAST - 2)

@@ -18,7 +18,7 @@ C_IN = 1024
 K_PASSES = C_IN // (P * PACK)
 UNITS = BATCH * HEADS
 ROW_TILES = PIX // P
-LAST_PAIR = UNITS // 2 - 1
+BY_DMA = [(u, u + 1) for u in range(0, UNITS - 4, 2)] + [(UNITS - 4,)]
 X_PIECE = 256
 LOADS_AHEAD = 4
 SCALE = 1.0 / DH**0.5
@@ -63,9 +63,11 @@ def tile_multiheadselfattention2d_pa_kernel(tc, vh, zh, r_pos, x, w_q, out):
 
         load_unit(0)
         load_w(0)
+        load_unit(1)
+        load_w(1)
         load_x(0, 0)
         load_x(0, 1)
-        for hd in range(1, LOADS_AHEAD):
+        for hd in range(2, LOADS_AHEAD):
             load_unit(hd)
             load_w(hd)
 
@@ -83,18 +85,15 @@ def tile_multiheadselfattention2d_pa_kernel(tc, vh, zh, r_pos, x, w_q, out):
         def regroup_x(b, g):
             grouped = stage.tile([P, PIX, PACK], BF16, name="x_grouped", align_bytes=64)
             flat = x_sb[b, g][:].rearrange("q t n -> q n t")
-            if (b, g) == (0, 0):
-                nc.vector.tensor_copy(out=grouped[:], in_=flat)
-            else:
-                for c in range(0, PIX, X_PIECE):
-                    nc.gpsimd.tensor_scalar(
-                        out=grouped[:, c : c + X_PIECE, :],
-                        in0=flat[:, c : c + X_PIECE, :],
-                        scalar1=1.0,
-                        scalar2=0.0,
-                        op0=ALU.mult,
-                        op1=ALU.add,
-                    )
+            for c in range(0, PIX, X_PIECE):
+                nc.gpsimd.tensor_scalar(
+                    out=grouped[:, c : c + X_PIECE, :],
+                    in0=flat[:, c : c + X_PIECE, :],
+                    scalar1=1.0,
+                    scalar2=0.0,
+                    op0=ALU.mult,
+                    op1=ALU.add,
+                )
             x_grouped[b, g] = grouped
 
         def quantise_x(b, g):
@@ -174,6 +173,12 @@ def tile_multiheadselfattention2d_pa_kernel(tc, vh, zh, r_pos, x, w_q, out):
             nc.tensor.matmul(out=s_ps[:], lhsT=vh_sb[i][:, queries], rhs=r_sb[hd][:], start=False, stop=True)
             s_banks[i, mt] = s_ps
 
+        def group_of(i):
+            for group in BY_DMA:
+                if i in group:
+                    return group[0], group.index(i)
+            return i, 0
+
         def max_rows(i, mt):
             s_ps = s_banks[i, mt]
             neg_scaled = ring.tile([P, PIX], F32, name="neg_scaled")
@@ -191,9 +196,11 @@ def tile_multiheadselfattention2d_pa_kernel(tc, vh, zh, r_pos, x, w_q, out):
 
         def exp_rows(i, mt):
             neg_scaled, shift = scaled[i, mt]
-            j, a = divmod(i, 2)
-            if a == 0 and mt == 0:
-                row_sum[j] = ring.tile([P, 2, ROW_TILES], F32, name="row_sum")
+            if mt == 0:
+                j, a = group_of(i)
+                if a == 0:
+                    row_sum[j] = ring.tile([P, 2, ROW_TILES], F32, name="row_sum", bufs=6)
+            j, a = group_of(i)
             if mt % 2 == 0:
                 e_rows[i, mt // 2] = ring.tile([P, 2, PIX], BF16, name="e_rows")
             nc.scalar.activation(
@@ -244,11 +251,14 @@ def tile_multiheadselfattention2d_pa_kernel(tc, vh, zh, r_pos, x, w_q, out):
             nc.gpsimd.memset(inv_tile[:], 0.0)
             inv_tiles.append(inv_tile)
 
-        def invert_sums(j, first=0, count=2 * ROW_TILES):
-            cols = slice(first, first + count)
-            inv_sums[j] = inv_tiles[j % 2]
+        def invert_sums(j, count):
+            if count == 2 or j == UNITS - 4:
+                inv_sums[j] = inv_tiles[(j // 2) % 2]
+            else:
+                inv_sums[j] = ring.tile([P, ROW_TILES], F32, name="inv_sum")
             nc.vector.reciprocal(
-                out=inv_sums[j][:, cols], in_=row_sum[j][:].rearrange("p a t -> p (a t)")[:, cols]
+                out=inv_sums[j][:, : count * ROW_TILES],
+                in_=row_sum[j][:].rearrange("p a t -> p (a t)")[:, : count * ROW_TILES],
             )
 
         def turn_sums(j):
@@ -256,36 +266,32 @@ def tile_multiheadselfattention2d_pa_kernel(tc, vh, zh, r_pos, x, w_q, out):
             nc.tensor.transpose(out=turned[:], in_=inv_sums[j][:], identity=ident_f32[:])
             inv_banks[j] = turned
 
-        def spread_by_dma(j):
+        def spread_by_dma(group):
+            count = len(group)
             rows_sb = ring.tile([2 * ROW_TILES, P], F32, name="inv_rows_sb")
-            nc.scalar.copy(out=rows_sb[:], in_=inv_banks[j][: 2 * ROW_TILES, :])
-            b, hd = divmod(2 * j, HEADS)
-            rows = out[b, hd * DH : hd * DH + 2].rearrange("c h w -> (c h w)")
-            nc.sync.dma_start(out=rows.rearrange("(k p) -> k p", p=P), in_=rows_sb[:])
+            nc.vector.tensor_copy(out=rows_sb[: count * ROW_TILES, :], in_=inv_banks[group[0]][: count * ROW_TILES, :])
+            b, hd = divmod(group[0], HEADS)
+            rows = out[b, hd * DH : hd * DH + count].rearrange("c h w -> (c h w)")
+            nc.sync.dma_start(out=rows.rearrange("(k p) -> k p", p=P), in_=rows_sb[: count * ROW_TILES, :])
             spread = ring.tile([P, 2, PIX], F32, name="spread")
             nc.sync.dma_start(
-                out=spread[:].rearrange("c a m -> c (a m)"), in_=rows.partition_broadcast(P)
+                out=spread[:, :count, :].rearrange("c a m -> c (a m)"), in_=rows.partition_broadcast(P)
             )
-            for a in range(2):
-                inv_rows[2 * j + a] = spread[:, a, :]
+            for u in group:
+                inv_rows[u] = spread[:, group.index(u), :]
 
-        def spread_by_transpose(i, first=0, count=ROW_TILES):
-            j, a = divmod(i, 2)
-            if first == 0:
-                row_banks[i] = psum_m.tile([P, PIX], F32, name="row_ps", tag="misc")
-            for mt in range(first, first + count):
-                col = a * ROW_TILES + mt
+        def spread_by_transpose(i):
+            row_banks[i] = psum_m.tile([P, PIX], F32, name="row_ps", tag="misc")
+            for mt in range(ROW_TILES):
                 nc.tensor.transpose(
                     out=row_banks[i][:, mt * P : (mt + 1) * P],
-                    in_=inv_sums[j][:, col : col + 1].to_broadcast([P, P]),
+                    in_=inv_sums[i][:, mt : mt + 1].to_broadcast([P, P]),
                     identity=ident_f32[:],
                 )
 
-        def copy_row(i, copy, first=0, count=ROW_TILES):
-            if first == 0:
-                inv_rows[i] = ring.tile([P, PIX], F32, name="inv_row")
-            cols = slice(first * P, (first + count) * P)
-            copy(out=inv_rows[i][:, cols], in_=row_banks[i][:, cols])
+        def copy_row(i, copy):
+            inv_rows[i] = ring.tile([P, PIX], F32, name="inv_row")
+            copy(out=inv_rows[i][:], in_=row_banks[i][:])
 
         o_banks = {}
 
@@ -328,11 +334,14 @@ def tile_multiheadselfattention2d_pa_kernel(tc, vh, zh, r_pos, x, w_q, out):
         PROJECT = {}
         for u in range(UNITS):
             if u < 6:
-                r = u + 2
+                r = u + 3
             else:
                 r = max(u, 8 + (u - 6) // 2)
             PROJECT.setdefault(r, []).append(u)
-        W_ROUND = {0: [0], 1: [1, 2], 2: [3], 3: [4], 4: [5], 5: [6], 6: [7]}
+        FINISH = {i: [i - 5] for i in range(5, LAST)}
+        FINISH[LAST] = [LAST - 5, LAST - 4]
+        W_ROUND = {i: [i + 1] for i in range(HEADS - 1)}
+        SPREAD = {group[-1] + 1: group for group in BY_DMA}
 
         with tc.manual_schedule():
             for i in range(UNITS):
@@ -344,29 +353,35 @@ def tile_multiheadselfattention2d_pa_kernel(tc, vh, zh, r_pos, x, w_q, out):
                     load_x(1, i)
 
                 scores(i, 0)
+                if i == 0:
+                    transpose_w(0)
                 if live(i - 1):
                     transpose_e(i - 1, 0, 2)
                 max_rows(i, 0)
                 if live(i - 2):
                     quantise_e(i - 2)
-                if i == 1:
-                    quantise_x(0, 0)
                 if live(i - 1):
                     copy_e(i - 1, 0, 2)
+                if i == 0:
+                    copy_w(0)
                 exp_rows(i, 0)
 
                 scores(i, 1)
                 for u in PROJECT.get(i, []):
                     project_values(u)
                 max_rows(i, 1)
+                if i in SPREAD:
+                    invert_sums(SPREAD[i][0], len(SPREAD[i]))
+                if i == 1:
+                    quantise_w(0)
                 for hd in W_ROUND.get(i - 1, []):
                     quantise_w(hd)
-                if i % 2 == 0 and i >= 2:
-                    invert_sums(i // 2 - 1)
-                if i == LAST:
-                    invert_sums(LAST_PAIR, 0, ROW_TILES)
+                if i in (LAST - 1, LAST):
+                    invert_sums(i - 1, 1)
                 if i in (4, 5):
                     quantise_x(1, i - 4)
+                if i in (1, 2):
+                    quantise_x(0, i - 1)
                 for u in PROJECT.get(i, []):
                     copy_q(u)
                 exp_rows(i, 1)
@@ -374,27 +389,21 @@ def tile_multiheadselfattention2d_pa_kernel(tc, vh, zh, r_pos, x, w_q, out):
                 scores(i, 2)
                 if live(i - 1):
                     transpose_e(i - 1, 2, 2)
-                if i % 2 == 0 and i >= 2:
-                    turn_sums(i // 2 - 1)
-                if i == LAST:
-                    spread_by_transpose(LAST - 1)
                 max_rows(i, 2)
                 if i == 0:
                     regroup_x(0, 0)
                     regroup_x(0, 1)
                 if i in (2, 3):
                     regroup_x(1, i - 2)
-                if i == 1:
-                    quantise_x(0, 1)
                 if live(i - 1):
                     copy_e(i - 1, 2, 2)
-                if i % 2 == 0 and i >= 2:
-                    spread_by_dma(i // 2 - 1)
                 exp_rows(i, 2)
 
                 scores(i, 3)
-                if live(i - 4):
-                    attend(i - 4)
+                for u in FINISH.get(i, []):
+                    attend(u)
+                if i in SPREAD:
+                    turn_sums(SPREAD[i][0])
                 for hd in W_ROUND.get(i, []):
                     transpose_w(hd)
                 max_rows(i, 3)
@@ -402,32 +411,36 @@ def tile_multiheadselfattention2d_pa_kernel(tc, vh, zh, r_pos, x, w_q, out):
                     quantise_q(u)
                 for hd in W_ROUND.get(i, []):
                     copy_w(hd)
-                if i == LAST:
-                    copy_row(LAST - 1, nc.scalar.copy)
                 exp_rows(i, 3)
-                if live(i - 4):
-                    finish(i - 4)
+                if i in SPREAD:
+                    spread_by_dma(SPREAD[i])
+                for u in FINISH.get(i, []):
+                    finish(u)
 
+            spread_by_transpose(LAST - 2)
             transpose_e(LAST, 0, 2)
             attend(LAST - 3)
             transpose_e(LAST, 2, 1)
+            spread_by_transpose(LAST - 1)
             quantise_e(LAST - 1)
+            copy_row(LAST - 2, nc.vector.tensor_copy)
             copy_e(LAST, 0, 2)
             copy_e(LAST, 2, 1)
-            invert_sums(LAST_PAIR, ROW_TILES, ROW_TILES)
+            copy_row(LAST - 1, nc.scalar.copy)
+            invert_sums(LAST, 1)
             attend(LAST - 2)
             attend(LAST - 1)
             transpose_e(LAST, 3, 1)
             spread_by_transpose(LAST)
             copy_e(LAST, 3, 1)
             copy_row(LAST, nc.scalar.copy)
-            finish(LAST - 1)
+            finish(LAST - 3)
             quantise_e(LAST, 0, 2 * P)
             quantise_e(LAST, 2 * P, 3 * P)
             quantise_e(LAST, 3 * P, 4 * P)
             attend(LAST, 0, 2 * P)
             attend(LAST, 2 * P, 3 * P)
             attend(LAST, 3 * P, 4 * P)
-            finish(LAST - 3)
-            finish(LAST)
             finish(LAST - 2)
+            finish(LAST - 1)
+            finish(LAST)

@@ -336,11 +336,11 @@ def tile_multiheadselfattention2d_pa_kernel(tc, vh, zh, r_pos, x, w_q, out):
             if u < 6:
                 r = u + 3
             else:
-                r = max(u, 8 + (u - 6) // 2)
+                r = max(u, 9 + (u - 6) // 2)
             PROJECT.setdefault(r, []).append(u)
         FINISH = {i: [i - 5] for i in range(5, LAST)}
         FINISH[LAST] = [LAST - 5, LAST - 4]
-        W_ROUND = {i: [i + 1] for i in range(HEADS - 1)}
+        W_ROUND = {i: [i] for i in range(1, HEADS)}
         SPREAD = {group[-1] + 1: group for group in BY_DMA}
 
         with tc.manual_schedule():
@@ -380,8 +380,8 @@ def tile_multiheadselfattention2d_pa_kernel(tc, vh, zh, r_pos, x, w_q, out):
                     invert_sums(i - 1, 1)
                 if i in (4, 5):
                     quantise_x(1, i - 4)
-                if i in (1, 2):
-                    quantise_x(0, i - 1)
+                if i == 2:
+                    quantise_x(0, 0)
                 for u in PROJECT.get(i, []):
                     copy_q(u)
                 exp_rows(i, 1)
@@ -407,6 +407,8 @@ def tile_multiheadselfattention2d_pa_kernel(tc, vh, zh, r_pos, x, w_q, out):
                 for hd in W_ROUND.get(i, []):
                     transpose_w(hd)
                 max_rows(i, 3)
+                if i == 2:
+                    quantise_x(0, 1)
                 for u in PROJECT.get(i, []):
                     quantise_q(u)
                 for hd in W_ROUND.get(i, []):
@@ -434,13 +436,13 @@ def tile_multiheadselfattention2d_pa_kernel(tc, vh, zh, r_pos, x, w_q, out):
             spread_by_transpose(LAST)
             copy_e(LAST, 3, 1)
             copy_row(LAST, nc.scalar.copy)
-            finish(LAST - 3)
             quantise_e(LAST, 0, 2 * P)
             quantise_e(LAST, 2 * P, 3 * P)
+            finish(LAST - 2)
             quantise_e(LAST, 3 * P, 4 * P)
             attend(LAST, 0, 2 * P)
             attend(LAST, 2 * P, 3 * P)
             attend(LAST, 3 * P, 4 * P)
-            finish(LAST - 2)
+            finish(LAST - 3)
             finish(LAST - 1)
             finish(LAST)

from contextlib import ExitStack

import concourse.mybir as mybir
from concourse.masks import make_identity

BF16 = mybir.dt.bfloat16
F32 = mybir.dt.float32
U32 = mybir.dt.uint32
U8 = mybir.dt.uint8
FP8X4 = mybir.dt.float8_e4m3fn_x4
ACT = mybir.ActivationFunctionType
ALU = mybir.AluOpType

P = 128
PACK = 4
BATCH, HEADS, DH, PIX = 2, 8, 128, 512
C_IN = 1024
K_PASSES = C_IN // (P * PACK)
UNITS = BATCH * HEADS
ROW_TILES = PIX // P
BY_DMA = [(u, u + 1) for u in range(0, UNITS - 4, 2)] + [(UNITS - 4,)]
X_PIECE = 256
LOADS_AHEAD = 4
SCALE = 1.0 / DH**0.5

FLOPS = 2 * UNITS * PIX * PIX * DH * 3 + 2 * BATCH * HEADS * DH * C_IN * PIX


def tile_multiheadselfattention2d_pa_kernel(tc, vh, zh, r_pos, x, w_q, out):
    nc = tc.nc
    with ExitStack() as ctx:
        consts = ctx.enter_context(tc.tile_pool(name="consts", bufs=1))
        inputs = ctx.enter_context(tc.tile_pool(name="inputs", bufs=1))
        kept = ctx.enter_context(tc.tile_pool(name="kept", bufs=1))
        stage = ctx.enter_context(tc.tile_pool(name="stage", bufs=3))
        ring = ctx.enter_context(tc.tile_pool(name="ring", bufs=4))
        psum_s = ctx.enter_context(tc.psum_pool(name="psum_s", bufs=3))
        psum_e = ctx.enter_context(tc.psum_pool(name="psum_e", bufs=2))
        psum_m = ctx.enter_context(tc.psum_pool(name="psum_m", bufs=3))

        vh_sb, zh_sb, r_sb, w_sb, x_sb = {}, {}, {}, {}, {}

        def load_unit(i):
            b, hd = divmod(i, HEADS)
            vh_sb[i] = inputs.tile([P, PIX], BF16, name="vh_sb%d" % i)
            nc.sync.dma_start(out=vh_sb[i][:], in_=vh[b, hd])
            zh_sb[i] = inputs.tile([P, PIX], BF16, name="zh_sb%d" % i)
            nc.sync.dma_start(out=zh_sb[i][:], in_=zh[b, hd])
            if b == 0:
                r_sb[hd] = inputs.tile([P, PIX], BF16, name="r_sb%d" % hd)
                nc.sync.dma_start(out=r_sb[hd][:], in_=r_pos[hd])

        def load_x(b, g):
            x_sb[b, g] = inputs.tile([P, PACK, PIX], BF16, name="x_sb%d_%d" % (b, g))
            nc.sync.dma_start(
                out=x_sb[b, g][:].rearrange("q (u e) n -> q u (e n)", e=2),
                in_=x[b, g * P * PACK : (g + 1) * P * PACK].rearrange("(u q e) h w -> q u (e h w)", u=2, e=2),
            )

        def load_w(hd):
            w_sb[hd] = inputs.tile([P, C_IN], BF16, name="w_sb%d" % hd)
            nc.sync.dma_start(out=w_sb[hd][:], in_=w_q[hd * DH : (hd + 1) * DH, :])

        load_unit(0)
        load_w(0)
        load_unit(1)
        load_w(1)
        load_x(0, 0)
        load_x(0, 1)
        for hd in range(2, LOADS_AHEAD):
            load_unit(hd)
            load_w(hd)

        ident_f32 = consts.tile([P, P], F32)
        make_identity(nc, ident_f32[:])
        warm = consts.tile([P, 1], F32)
        nc.vector.memset(warm[:], 0.0)
        warm_out = consts.tile([P, 1], F32)
        nc.scalar.activation(out=warm_out[:], in_=warm[:], func=ACT.Exp)

        x_codes = kept.tile([P, BATCH, K_PASSES, PIX], U32, align_bytes=64)
        x_scales = kept.tile([P, BATCH, K_PASSES, PIX], U8, align_bytes=64)
        x_grouped = {}

        def regroup_x(b, g):
            grouped = stage.tile([P, PIX, PACK], BF16, name="x_grouped", align_bytes=64)
            flat = x_sb[b, g][:].rearrange("q t n -> q n t")
            for c in range(0, PIX, X_PIECE):
                nc.gpsimd.tensor_scalar(
                    out=grouped[:, c : c + X_PIECE, :],
                    in0=flat[:, c : c + X_PIECE, :],
                    scalar1=1.0,
                    scalar2=0.0,
                    op0=ALU.mult,
                    op1=ALU.add,
                )
            x_grouped[b, g] = grouped

        def quantise_x(b, g):
            nc.vector.quantize_mx(
                out=x_codes[:, b, g, :].bitcast(FP8X4),
                scales=x_scales[:, b, g, :],
                in_=x_grouped[b, g][:].rearrange("q n t -> q (n t)"),
            )

        w_codes = kept.tile([P, HEADS, K_PASSES, DH], U32, align_bytes=64)
        w_scales = kept.tile([P, HEADS, K_PASSES, DH], U8, align_bytes=64)
        w_banks, w_grouped = {}, {}

        def transpose_w(hd):
            w_words = w_sb[hd][:].bitcast(F32)
            wT_ps = psum_m.tile([P, K_PASSES, 2, DH], F32, name="wT_ps", tag="misc")
            for g in range(K_PASSES):
                for u in range(2):
                    first = (2 * g + u) * P
                    nc.tensor.transpose(
                        out=wT_ps[:, g, u, :], in_=w_words[:, first : first + P], identity=ident_f32[:]
                    )
            w_banks[hd] = wT_ps

        def copy_w(hd):
            w_grouped[hd] = stage.tile([P, K_PASSES, DH, PACK], BF16, name="w_grouped", align_bytes=64)
            nc.scalar.copy(
                out=w_grouped[hd][:].bitcast(F32), in_=w_banks[hd][:].rearrange("q g u c -> q g c u")
            )

        def quantise_w(hd):
            nc.vector.quantize_mx(
                out=w_codes[:, hd].rearrange("q g c -> q (g c)").bitcast(FP8X4),
                scales=w_scales[:, hd].rearrange("q g c -> q (g c)"),
                in_=w_grouped[hd][:].rearrange("q g c t -> q (g c t)"),
            )

        q_banks, q_grouped, q_codes, q_scales = {}, {}, {}, {}

        def project_values(i):
            b, hd = divmod(i, HEADS)
            qT_ps = psum_m.tile([P, PACK, DH], F32, name="qT_ps", tag="misc")
            for t in range(PACK):
                pixels = slice(t * P, (t + 1) * P)
                for g in range(K_PASSES):
                    nc.tensor.matmul_mx(
                        out=qT_ps[:, t, :],
                        lhsT=x_codes[:, b, g, pixels].bitcast(FP8X4),
                        lhsT_scale=x_scales[:, b, g, pixels],
                        rhs=w_codes[:, hd, g, :].bitcast(FP8X4),
                        rhs_scale=w_scales[:, hd, g, :],
                        start=(g == 0),
                        stop=(g == K_PASSES - 1),
                    )
            q_banks[i] = qT_ps

        def copy_q(i):
            q_grouped[i] = stage.tile([P, DH, PACK], BF16, name="q_grouped", align_bytes=64)
            nc.scalar.copy(out=q_grouped[i][:], in_=q_banks[i][:].rearrange("p t d -> p d t"))

        def quantise_q(i):
            q_codes[i] = ring.tile([P, DH], U32, name="q_codes", bufs=6, align_bytes=64)
            q_scales[i] = ring.tile([P, DH], U8, name="q_scales", bufs=6, align_bytes=64)
            nc.vector.quantize_mx(
                out=q_codes[i][:].bitcast(FP8X4),
                scales=q_scales[i][:],
                in_=q_grouped[i][:].rearrange("p d t -> p (d t)"),
            )

        s_banks, scaled, e_rows, row_sum = {}, {}, {}, {}

        def scores(i, mt):
            hd = i % HEADS
            queries = slice(mt * P, (mt + 1) * P)
            s_ps = psum_s.tile([P, PIX], F32, name="s_ps")
            nc.tensor.matmul(out=s_ps[:], lhsT=vh_sb[i][:, queries], rhs=zh_sb[i][:], start=True, stop=False)
            nc.tensor.matmul(out=s_ps[:], lhsT=vh_sb[i][:, queries], rhs=r_sb[hd][:], start=False, stop=True)
            s_banks[i, mt] = s_ps

        def group_of(i):
            for group in BY_DMA:
                if i in group:
                    return group[0], group.index(i)
            return i, 0

        def max_rows(i, mt):
            s_ps = s_banks[i, mt]
            neg_scaled = ring.tile([P, PIX], F32, name="neg_scaled")
            shift = ring.tile([P, 1], F32, name="shift")
            scaled[i, mt] = neg_scaled, shift
            nc.vector.tensor_scalar(
                out=neg_scaled[:],
                in0=s_ps[:],
                scalar1=-SCALE,
                scalar2=None,
                op0=ALU.mult,
                op1=ALU.min,
                accum_out=shift[:],
            )

        def exp_rows(i, mt):
            neg_scaled, shift = scaled[i, mt]
            if mt == 0:
                j, a = group_of(i)
                if a == 0:
                    row_sum[j] = ring.tile([P, 2, ROW_TILES], F32, name="row_sum", bufs=6)
            j, a = group_of(i)
            if mt % 2 == 0:
                e_rows[i, mt // 2] = ring.tile([P, 2, PIX], BF16, name="e_rows")
            nc.scalar.activation(
                out=e_rows[i, mt // 2][:, mt % 2, :].rearrange("m (u q e) -> m u q e", u=2, e=2),
                in_=neg_scaled[:].rearrange("m (u e q) -> m u q e", u=2, e=2),
                func=ACT.Exp,
                bias=shift[:],
                scale=-1.0,
                accum_out=row_sum[j][:, a, mt : mt + 1],
            )

        eT_banks, e_grouped, e_codes, e_scales = {}, {}, {}, {}

        def transpose_e(i, first, count):
            eT_ps = psum_e.tile([P, 2, count * P], F32, name="eT_ps")
            for mt in range(first, first + count):
                e_words = e_rows[i, mt // 2][:, mt % 2, :].bitcast(F32)
                cols = slice((mt - first) * P, (mt - first + 1) * P)
                for u in range(2):
                    nc.tensor.transpose(
                        out=eT_ps[:, u, cols], in_=e_words[:, u * P : (u + 1) * P], identity=ident_f32[:]
                    )
            eT_banks[i, first] = eT_ps

        def copy_e(i, first, count):
            if first == 0:
                e_grouped[i] = stage.tile([P, PIX, PACK], BF16, name="e_grouped", align_bytes=64)
            nc.scalar.copy(
                out=e_grouped[i][:, first * P : (first + count) * P, :].bitcast(F32),
                in_=eT_banks[i, first][:].rearrange("q u m -> q m u"),
            )

        def quantise_e(i, first=0, last=PIX):
            if first == 0:
                e_codes[i] = ring.tile([P, PIX], U32, name="e_codes", bufs=6, align_bytes=64)
                e_scales[i] = ring.tile([P, PIX], U8, name="e_scales", bufs=6, align_bytes=64)
            nc.vector.quantize_mx(
                out=e_codes[i][:, first:last].bitcast(FP8X4),
                scales=e_scales[i][:, first:last],
                in_=e_grouped[i][:, first:last, :].rearrange("p m t -> p (m t)"),
            )

        inv_sums, inv_banks, row_banks, inv_rows = {}, {}, {}, {}

        inv_tiles = []
        for k in range(2):
            inv_tile = consts.tile([P, P], F32, name="inv_tile%d" % k)
            nc.gpsimd.memset(inv_tile[:], 0.0)
            inv_tiles.append(inv_tile)

        def invert_sums(j, count):
            if count == 2 or j == UNITS - 4:
                inv_sums[j] = inv_tiles[(j // 2) % 2]
            else:
                inv_sums[j] = ring.tile([P, ROW_TILES], F32, name="inv_sum")
            nc.vector.reciprocal(
                out=inv_sums[j][:, : count * ROW_TILES],
                in_=row_sum[j][:].rearrange("p a t -> p (a t)")[:, : count * ROW_TILES],
            )

        def turn_sums(j):
            turned = psum_m.tile([P, P], F32, name="inv_turned", tag="misc")
            nc.tensor.transpose(out=turned[:], in_=inv_sums[j][:], identity=ident_f32[:])
            inv_banks[j] = turned

        def spread_by_dma(group):
            count = len(group)
            rows_sb = ring.tile([2 * ROW_TILES, P], F32, name="inv_rows_sb")
            nc.vector.tensor_copy(out=rows_sb[: count * ROW_TILES, :], in_=inv_banks[group[0]][: count * ROW_TILES, :])
            b, hd = divmod(group[0], HEADS)
            rows = out[b, hd * DH : hd * DH + count].rearrange("c h w -> (c h w)")
            nc.sync.dma_start(out=rows.rearrange("(k p) -> k p", p=P), in_=rows_sb[: count * ROW_TILES, :])
            spread = ring.tile([P, 2, PIX], F32, name="spread")
            nc.sync.dma_start(
                out=spread[:, :count, :].rearrange("c a m -> c (a m)"), in_=rows.partition_broadcast(P)
            )
            for u in group:
                inv_rows[u] = spread[:, group.index(u), :]

        def spread_by_transpose(i):
            row_banks[i] = psum_m.tile([P, PIX], F32, name="row_ps", tag="misc")
            for mt in range(ROW_TILES):
                nc.tensor.transpose(
                    out=row_banks[i][:, mt * P : (mt + 1) * P],
                    in_=inv_sums[i][:, mt : mt + 1].to_broadcast([P, P]),
                    identity=ident_f32[:],
                )

        def copy_row(i, copy):
            inv_rows[i] = ring.tile([P, PIX], F32, name="inv_row")
            copy(out=inv_rows[i][:], in_=row_banks[i][:])

        o_banks = {}

        def attend(i, first=0, last=PIX):
            if first == 0 and i < UNITS - 3:
                o_banks[i] = psum_m.tile([P, PIX], F32, name="o_ps", tag="misc")
            elif first == 0:
                o_banks[i] = psum_s.tile([P, PIX], F32, name="s_ps")
            nc.tensor.matmul_mx(
                out=o_banks[i][:, first:last],
                lhsT=q_codes[i][:].bitcast(FP8X4),
                lhsT_scale=q_scales[i][:],
                rhs=e_codes[i][:, first:last].bitcast(FP8X4),
                rhs_scale=e_scales[i][:, first:last],
                start=True,
                stop=True,
            )

        out_sb = {}

        def finish(i, first=0, last=PIX):
            b, hd = divmod(i, HEADS)
            if first == 0:
                out_sb[i] = ring.tile([P, PIX], F32, name="out_sb", bufs=6)
            nc.vector.tensor_tensor(
                out=out_sb[i][:, first:last],
                in0=o_banks[i][:, first:last],
                in1=inv_rows[i][:, first:last],
                op=ALU.mult,
            )
            nc.sync.dma_start(
                out=out[b, hd * DH : (hd + 1) * DH].rearrange("c h w -> c (h w)")[:, first:last],
                in_=out_sb[i][:, first:last],
            )

        def live(u):
            return 0 <= u < UNITS

        LAST = UNITS - 1
        PROJECT = {}
        for u in range(UNITS):
            if u < 6:
                r = u + 3
            else:
                r = max(u, 9 + (u - 6) // 2)
            PROJECT.setdefault(r, []).append(u)
        FINISH = {i: [i - 5] for i in range(5, LAST)}
        FINISH[LAST] = [LAST - 5, LAST - 4]
        W_ROUND = {i: [i] for i in range(1, HEADS)}
        SPREAD = {group[-1] + 1: group for group in BY_DMA}

        with tc.manual_schedule():
            for i in range(UNITS):
                if i + LOADS_AHEAD < UNITS:
                    load_unit(i + LOADS_AHEAD)
                if i + LOADS_AHEAD < HEADS:
                    load_w(i + LOADS_AHEAD)
                if i < K_PASSES:
                    load_x(1, i)

                scores(i, 0)
                if i == 0:
                    transpose_w(0)
                if live(i - 1):
                    transpose_e(i - 1, 0, 2)
                max_rows(i, 0)
                if live(i - 2):
                    quantise_e(i - 2)
                if live(i - 1):
                    copy_e(i - 1, 0, 2)
                if i == 0:
                    copy_w(0)
                exp_rows(i, 0)

                scores(i, 1)
                for u in PROJECT.get(i, []):
                    project_values(u)
                max_rows(i, 1)
                if i in SPREAD:
                    invert_sums(SPREAD[i][0], len(SPREAD[i]))
                if i == 1:
                    quantise_w(0)
                for hd in W_ROUND.get(i - 1, []):
                    quantise_w(hd)
                if i in (LAST - 1, LAST):
                    invert_sums(i - 1, 1)
                if i in (4, 5):
                    quantise_x(1, i - 4)
                if i == 2:
                    quantise_x(0, 0)
                for u in PROJECT.get(i, []):
                    copy_q(u)
                exp_rows(i, 1)

                scores(i, 2)
                if live(i - 1):
                    transpose_e(i - 1, 2, 2)
                max_rows(i, 2)
                if i == 0:
                    regroup_x(0, 0)
                    regroup_x(0, 1)
                if i in (2, 3):
                    regroup_x(1, i - 2)
                if live(i - 1):
                    copy_e(i - 1, 2, 2)
                exp_rows(i, 2)

                scores(i, 3)
                for u in FINISH.get(i, []):
                    attend(u)
                if i in SPREAD:
                    turn_sums(SPREAD[i][0])
                for hd in W_ROUND.get(i, []):
                    transpose_w(hd)
                max_rows(i, 3)
                if i == 2:
                    quantise_x(0, 1)
                for u in PROJECT.get(i, []):
                    quantise_q(u)
                for hd in W_ROUND.get(i, []):
                    copy_w(hd)
                exp_rows(i, 3)
                if i in SPREAD:
                    spread_by_dma(SPREAD[i])
                for u in FINISH.get(i, []):
                    finish(u)

            spread_by_transpose(LAST - 2)
            transpose_e(LAST, 0, 2)
            attend(LAST - 3)
            transpose_e(LAST, 2, 1)
            spread_by_transpose(LAST - 1)
            quantise_e(LAST - 1)
            copy_row(LAST - 2, nc.vector.tensor_copy)
            copy_e(LAST, 0, 2)
            copy_e(LAST, 2, 1)
            copy_row(LAST - 1, nc.scalar.copy)
            invert_sums(LAST, 1)
            attend(LAST - 2)
            attend(LAST - 1)
            transpose_e(LAST, 3, 1)
            spread_by_transpose(LAST)
            copy_e(LAST, 3, 1)
            copy_row(LAST, nc.scalar.copy)
            quantise_e(LAST, 0, 2 * P)
            quantise_e(LAST, 2 * P, 3 * P)
            finish(LAST - 2)
            quantise_e(LAST, 3 * P, 4 * P)
            attend(LAST, 0, 2 * P)
            attend(LAST, 2 * P, 3 * P)
            attend(LAST, 3 * P, 4 * P)
            finish(LAST - 3)
            finish(LAST - 1)
            finish(LAST)
